import numpy as np
import ml_dtypes


def mxq(x, axis, fmt="e4m3"):
    dtype, down = {"e4m3": (ml_dtypes.float8_e4m3fn, 7), "e5m2": (ml_dtypes.float8_e5m2, 14)}[fmt]
    v = np.moveaxis(np.asarray(x, np.float32).astype(ml_dtypes.bfloat16).astype(np.float64), axis, -1)
    blocks = v.reshape(v.shape[:-1] + (-1, 32))
    amax = np.abs(blocks).max(-1, keepdims=True)
    byte = np.maximum(np.where(amax > 0, np.frexp(amax)[1] - 1 + 127, 0) - down, 1)
    scale = np.exp2(byte - 127.0)
    codes = (blocks / scale).astype(np.float32).astype(dtype).astype(np.float64)
    return np.moveaxis((codes * scale).reshape(v.shape), -1, axis)


WIDE = False


def mx_kscale(k):
    if not WIDE:
        return np.ones(k)
    levels = np.array([10, -10, 5, -5, 0])
    a = np.random.permutation(np.resize(levels, k // 512 * 4)).reshape(k // 512, 4)
    idx = np.arange(k)
    return np.exp2(a[idx // 512, idx % 128 // 32])


BF16 = ml_dtypes.bfloat16


def bf(x):
    return np.asarray(x, np.float32).astype(BF16)


def f64(x):
    return np.asarray(x).astype(np.float64)


B, L, E, H = 8, 512, 512, 128


def skew(m):
    mp = np.pad(m, ((0, 0), (0, 0), (1, 0)))
    return mp.reshape(B, L + 1, L)[:, 1:, :]


def setup_inputs():
    s = mx_kscale(E)
    return {"x": bf(np.random.standard_normal((B, L, E)) * s),
            "q": bf(np.random.standard_normal((B, L, H)) * 1.5),
            "k": bf(np.random.standard_normal((B, L, H))),
            "Wv": bf(np.random.standard_normal((H, E)) / np.sqrt(E) / s[None, :]),
            "rel_emb": bf(np.random.standard_normal((L, H)) / np.sqrt(H))}


def reference(x, q, k, Wv, rel_emb):
    v = mxq(f64(x), 2, "e4m3") @ mxq(f64(Wv), 1, "e4m3").T
    sc = f64(q) @ f64(k).transpose(0, 2, 1) / np.sqrt(H)
    sc = sc + skew(f64(q) @ f64(rel_emb).T)
    causal = np.tril(np.ones((L, L), dtype=bool))
    sc = np.where(causal[None], sc, -np.inf)
    e = np.exp(sc - sc.max(-1, keepdims=True))
    return (mxq(e, 2, "e4m3") @ mxq(v, 1, "e4m3")) / e.sum(-1, keepdims=True)

@@ -1,0 +1,388 @@
+import math
+from contextlib import ExitStack
+
+import concourse.mybir as mybir
+from concourse.masks import make_identity
+
+F32 = mybir.dt.float32
+BF16 = mybir.dt.bfloat16
+U32 = mybir.dt.uint32
+U8 = mybir.dt.uint8
+FP8X4 = mybir.dt.float8_e4m3fn_x4
+ALU = mybir.AluOpType
+ACT = mybir.ActivationFunctionType
+AXIS = mybir.AxisListType
+
+B, L, E, H = 8, 512, 512, 128
+P = 128
+PACK = 4
+NBLK = L // P
+BANK = 512
+
+FLOPS = 4 * 2 * B * L * L * H
+
+WIDTH = {0: 128, 1: 256, 2: 384, 3: 512}
+BANKS = ((3,), (2, 0), (1,))
+COL0 = {3: 0, 2: 512, 0: 896, 1: 1024}
+ROW = 1280
+PAD = 8
+GROUPS = ((0, 1), (2, 3, 4), (5, 6, 7))
+assert P * (3 * ROW + PAD) <= B * L * H
+
+MASKED = -1.0e30
+SCALE = 1.0 / math.sqrt(H)
+
+FIRST_STORE = 4
+
+
+def tile_relativeattentionhead_pa_kernel(tc, x, q, k, Wv, rel_emb, out):
+    nc = tc.nc
+    out_flat = out.rearrange("b l h -> (b l h)")
+
+    with ExitStack() as ctx:
+        keep = ctx.enter_context(tc.tile_pool(name="keep", bufs=1))
+        work = ctx.enter_context(tc.tile_pool(name="work", bufs=2))
+        small = ctx.enter_context(tc.tile_pool(name="small", bufs=4))
+        ctx.enter_context(tc.manual_schedule())
+
+        ident_bf = keep.tile([P, P], BF16)
+        ident_f32 = keep.tile([P, P], F32)
+        mask_f32 = keep.tile([P, P], F32)
+        mask_bf = keep.tile([P, P], BF16)
+        rel_sb = keep.tile([P, NBLK, H], BF16)
+        wv_sb = keep.tile([P, E], BF16)
+        q_sb = keep.tile([P, B * NBLK, H], BF16)
+        k_sb = keep.tile([P, B * NBLK, H], BF16)
+        x_sb = keep.tile([P, B * NBLK, E], BF16)
+        relT = keep.tile([P, L], BF16)
+        qT = [keep.tile([P, L], BF16, name="qT%d" % b) for b in range(B)]
+        kT = [keep.tile([P, L], BF16, name="kT%d" % b) for b in range(B)]
+        m_rows = [keep.tile([P, len(GROUPS[g]) * ROW + PAD], F32, name="m_rows%d" % g) for g in range(len(GROUPS))]
+        s_sb = [keep.tile([P, ROW], F32, name="s_sb%d" % b) for b in range(B)]
+        e_grouped = keep.tile([P, NBLK * P * PACK], BF16, align_bytes=64)
+        out_sb = keep.tile([P, B * NBLK, H], F32)
+
+        make_identity(nc, ident_bf[:])
+        nc.gpsimd.memset(mask_f32[:], 0.0)
+        nc.gpsimd.affine_select(
+            out=mask_f32[:],
+            in_=mask_f32[:],
+            compare_op=ALU.is_ge,
+            fill=MASKED,
+            base=0,
+            pattern=[[-1, P]],
+            channel_multiplier=1,
+        )
+        make_identity(nc, ident_f32[:])
+        for rows in m_rows:
+            nc.vector.memset(rows[:, rows.shape[1] - PAD :], 0.0)
+        nc.vector.memset(e_grouped[:], 0.0)
+        nc.vector.tensor_copy(out=mask_bf[:], in_=mask_f32[:])
+
+        def load_tokens(dst, src, first, stop):
+            nc.sync.dma_start(
+                out=dst[:, first * NBLK : stop * NBLK, :],
+                in_=src[first:stop].rearrange("b (g p) f -> p (b g) f", p=P),
+            )
+
+        def copy_out(piece, dst, src):
+            if piece % 2 == 0:
+                nc.scalar.copy(out=dst, in_=src)
+            else:
+                nc.vector.tensor_copy(out=dst, in_=src)
+
+        def quantise(bf16_tile, pool, width, name):
+            words = pool.tile([P, width], U32, name=name + "_words", align_bytes=64)
+            scales = pool.tile([P, width], U8, name=name + "_scales", align_bytes=64)
+            nc.vector.quantize_mx(out=words[:].bitcast(FP8X4), scales=scales[:], in_=bf16_tile)
+            return words, scales
+
+        def flip_tokens(pool, src):
+            flipped = pool.tile([P, NBLK, P], BF16, tag="flip")
+            for g in range(NBLK):
+                nc.tensor.transpose(flipped[:, g, :], src[:, g, :], ident_bf[:])
+            return flipped
+
+        def unload_tokens(dst, flipped):
+            nc.vector.tensor_copy(out=dst, in_=flipped[:].rearrange("p g r -> p (g r)"))
+
+        def flip_features(src_words, n_groups):
+            flipped = ps_flip.tile([P, n_groups, 2, P], F32, tag="flip")
+            for g in range(n_groups):
+                for u in range(2):
+                    nc.tensor.transpose(flipped[:, g, u, :], src_words[:, g, u * P : (u + 1) * P], ident_f32[:])
+            return flipped
+
+        def unload_features(dst_words, flipped):
+            nc.scalar.copy(out=dst_words, in_=flipped[:].rearrange("p g u r -> p g r u"))
+
+        def rel_products(pool, g, j):
+            b = GROUPS[g][j]
+            for bank, blocks in enumerate(BANKS):
+                first = COL0[blocks[0]]
+                m_ps = pool.tile([P, BANK], F32, tag="flip")
+                for blk in blocks:
+                    lo = COL0[blk] - first
+                    nc.tensor.matmul(
+                        m_ps[:, lo : lo + WIDTH[blk]],
+                        lhsT=qT[b][:, blk * P : (blk + 1) * P],
+                        rhs=relT[:, L - WIDTH[blk] : L],
+                        start=True,
+                        stop=True,
+                    )
+                width = sum(WIDTH[blk] for blk in blocks)
+                copy_out(
+                    bank,
+                    m_rows[g][:, j * ROW + first : j * ROW + first + width],
+                    m_ps[:, 0:width],
+                )
+
+        def make_rows(pool, g):
+            for b in GROUPS[g]:
+                unload_tokens(qT[b][:], flip_tokens(pool, q_sb[:, b * NBLK : (b + 1) * NBLK, :]))
+            for j in range(len(GROUPS[g])):
+                rel_products(pool, g, j)
+
+        def store_rows(g):
+            pitch = len(GROUPS[g]) * ROW + PAD
+            nc.sync.dma_start(out=out_flat[0 : P * pitch].rearrange("(p c) -> p c", c=pitch), in_=m_rows[g][:])
+
+        def read_back(g):
+            pitch = len(GROUPS[g]) * ROW + PAD
+            shifted = out_flat[P - 1 : P - 1 + P * (pitch - 1)].rearrange("(p c) -> p c", c=pitch - 1)
+            for j, b in enumerate(GROUPS[g]):
+                nc.sync.dma_start(out=s_sb[b][:], in_=shifted[:, j * ROW : (j + 1) * ROW])
+
+        x_flipped = {}
+        x_mx = {}
+        v_ps = {}
+        v_mx = {}
+        qk_ps = {}
+        e_sb = {}
+        eT_ps = {}
+        e_mx = {}
+        o_ps = {}
+        neg_max = {}
+        row_sum = {}
+
+        def flip_x(b):
+            src = x_sb[:].bitcast(F32)[:, b * NBLK : (b + 1) * NBLK, :]
+            x_flipped[b] = [flip_features(src[:, 2 * half : 2 * half + 2, :], 2) for half in range(2)]
+
+        def unload_x(b):
+            x_grouped = work.tile([P, L * PACK], BF16, align_bytes=64)
+            dst = x_grouped[:].bitcast(F32).rearrange("p (g r u) -> p g r u", g=NBLK, u=2)
+            for half in range(2):
+                unload_features(dst[:, 2 * half : 2 * half + 2], x_flipped[b][half])
+            return x_grouped
+
+        def project(b):
+            v_ps[b] = ps_mx.tile([P, NBLK, H], F32, name="v_ps", tag="mx")
+            x_words, x_scales = x_mx[b]
+            for t in range(NBLK):
+                nc.tensor.matmul_mx(
+                    out=v_ps[b][:, t, :],
+                    lhsT=x_words[:, t * P : (t + 1) * P].bitcast(FP8X4),
+                    lhsT_scale=x_scales[:, t * P : (t + 1) * P],
+                    rhs=wv_words[:].bitcast(FP8X4),
+                    rhs_scale=wv_scales[:],
+                    start=True,
+                    stop=True,
+                )
+
+        def unload_v(b):
+            v_grouped = work.tile([P, H * PACK], BF16, align_bytes=64)
+            nc.scalar.copy(
+                out=v_grouped[:].rearrange("p (h t) -> p h t", t=PACK),
+                in_=v_ps[b][:].rearrange("p t h -> p h t"),
+            )
+            return v_grouped
+
+        def scores(b, bank):
+            blocks = BANKS[bank]
+            first = COL0[blocks[0]]
+            qk_ps[b, bank] = ps_score.tile([P, BANK], F32, name="qk_ps", tag="score")
+            for blk in blocks:
+                lo = COL0[blk] - first
+                queries = qT[b][:, blk * P : (blk + 1) * P]
+                if blk > 0:
+                    nc.tensor.matmul(
+                        qk_ps[b, bank][:, lo : lo + blk * P],
+                        lhsT=queries,
+                        rhs=kT[b][:, 0 : blk * P],
+                        start=True,
+                        stop=True,
+                    )
+                diagonal = qk_ps[b, bank][:, lo + blk * P : lo + (blk + 1) * P]
+                nc.tensor.matmul(diagonal, lhsT=queries, rhs=kT[b][:, blk * P : (blk + 1) * P], start=True, stop=False)
+                nc.tensor.matmul(diagonal, lhsT=ident_bf[:], rhs=mask_bf[:], start=False, stop=True)
+
+        def add_rel(b, bank):
+            blocks = BANKS[bank]
+            first = COL0[blocks[0]]
+            width = sum(WIDTH[blk] for blk in blocks)
+            if bank == 0:
+                neg_max[b] = small.tile([P, NBLK], F32, name="neg_max")
+            nc.vector.scalar_tensor_tensor(
+                out=s_sb[b][:, first : first + width],
+                in0=qk_ps[b, bank][:, 0:width],
+                scalar=SCALE,
+                in1=s_sb[b][:, first : first + width],
+                op0=ALU.mult,
+                op1=ALU.add,
+            )
+
+        def row_max(b, bank):
+            for blk in BANKS[bank]:
+                nc.vector.tensor_reduce(
+                    out=neg_max[b][:, blk : blk + 1],
+                    in_=s_sb[b][:, COL0[blk] : COL0[blk] + WIDTH[blk]],
+                    axis=AXIS.X,
+                    op=ALU.max,
+                    negate=True,
+                )
+
+        def exponentiate(b):
+            e_sb[b] = work.tile([P, ROW], BF16, name="e_sb")
+            row_sum[b] = small.tile([P, NBLK], F32, name="row_sum")
+            eT_ps[b] = [
+                ps_eT.tile([P, 4, P], BF16, name="eT_even"),
+                ps_eT.tile([P, 6, P], BF16, name="eT_odd"),
+            ]
+            for blocks in BANKS:
+                for blk in blocks:
+                    cols = slice(COL0[blk], COL0[blk] + WIDTH[blk])
+                    nc.scalar.activation(
+                        out=e_sb[b][:, cols],
+                        in_=s_sb[b][:, cols],
+                        func=ACT.Exp,
+                        bias=neg_max[b][:, blk : blk + 1],
+                        scale=1.0,
+                        accum_out=row_sum[b][:, blk : blk + 1],
+                    )
+                    for t in range(blk + 1):
+                        nc.tensor.transpose(
+                            eT_ps[b][blk % 2][:, first_plane(blk) + t, :],
+                            e_sb[b][:, COL0[blk] + t * P : COL0[blk] + (t + 1) * P],
+                            ident_bf[:],
+                        )
+
+        def first_plane(blk):
+            return 0 if blk >= 2 else blk + 3
+
+        def unload_e(b):
+            for blocks in BANKS:
+                for blk in blocks:
+                    places = e_grouped[:, blk * P * PACK : (blk + 1) * P * PACK]
+                    planes = eT_ps[b][blk % 2][:, first_plane(blk) : first_plane(blk) + blk + 1, :]
+                    nc.scalar.copy(
+                        out=places.rearrange("p (i t) -> p i t", t=PACK)[:, :, 0 : blk + 1],
+                        in_=planes.rearrange("p t i -> p i t"),
+                    )
+
+        def weighted_sum(b):
+            o_ps[b] = ps_mx.tile([P, NBLK, H], F32, name="o_ps", tag="mx")
+            e_words, e_scales = e_mx[b]
+            v_words, v_scales = v_mx[b]
+            for blk in range(NBLK):
+                nc.tensor.matmul_mx(
+                    out=o_ps[b][:, blk, :],
+                    lhsT=e_words[:, blk * P : (blk + 1) * P].bitcast(FP8X4),
+                    lhsT_scale=e_scales[:, blk * P : (blk + 1) * P],
+                    rhs=v_words[:].bitcast(FP8X4),
+                    rhs_scale=v_scales[:],
+                    start=True,
+                    stop=True,
+                )
+
+        def normalise(b):
+            inv_sum = small.tile([P, NBLK], F32)
+            nc.vector.reciprocal(out=inv_sum[:], in_=row_sum[b][:])
+            nc.vector.tensor_tensor(
+                out=out_sb[:, b * NBLK : (b + 1) * NBLK, :],
+                in0=o_ps[b][:],
+                in1=inv_sum[:].unsqueeze(2).to_broadcast([P, NBLK, H]),
+                op=ALU.mult,
+            )
+
+        def store(first, stop):
+            nc.sync.dma_start(
+                out=out[first:stop].rearrange("b (g p) h -> p (b g) h", p=P),
+                in_=out_sb[:, first * NBLK : stop * NBLK, :],
+            )
+
+        def live(b):
+            return 0 <= b < B
+
+        def step(n):
+            if live(n - 1):
+                unload_e(n - 1)
+                v_grouped = unload_v(n - 1)
+            for bank in range(len(BANKS)):
+                if live(n):
+                    add_rel(n, bank)
+                    if bank > 0:
+                        row_max(n, bank - 1)
+                ahead = bank + 2
+                if live(n + ahead // len(BANKS)):
+                    scores(n + ahead // len(BANKS), ahead % len(BANKS))
+            if live(n + 2):
+                k_flipped = flip_tokens(ps_flip, k_sb[:, (n + 2) * NBLK : (n + 3) * NBLK, :])
+            if live(n - 1):
+                e_mx[n - 1] = quantise(e_grouped[:], work, L, "e")
+                v_mx[n - 1] = quantise(v_grouped[:], work, H, "v")
+                weighted_sum(n - 1)
+            if live(n):
+                row_max(n, len(BANKS) - 1)
+                x_grouped = unload_x(n)
+                exponentiate(n)
+            if live(n + 1):
+                flip_x(n + 1)
+            if live(n + 2):
+                unload_tokens(kT[n + 2][:], k_flipped)
+            if live(n):
+                x_mx[n] = quantise(x_grouped[:], work, L, "x")
+            if live(n - 1):
+                normalise(n - 1)
+                if n - 1 == FIRST_STORE:
+                    store(0, n)
+                elif n - 1 > FIRST_STORE:
+                    store(n - 1, n)
+            if live(n):
+                project(n)
+
+        nc.sync.dma_start(out=rel_sb[:], in_=rel_emb.rearrange("(g p) h -> p g h", p=P))
+        load_tokens(q_sb, q, 0, 2)
+        load_tokens(q_sb, q, 2, B)
+        load_tokens(k_sb, k, 0, 2)
+        nc.sync.dma_start(out=wv_sb[:], in_=Wv)
+
+        def load_next(i):
+            load_tokens(x_sb, x, i, i + 1)
+            load_tokens(k_sb, k, i + 2, i + 3)
+
+        with tc.psum_pool(name="ps_head", bufs=8) as ps_head:
+            unload_tokens(relT[:], flip_tokens(ps_head, rel_sb))
+            for g in range(len(GROUPS)):
+                make_rows(ps_head, g)
+                store_rows(g)
+                load_next(2 * g)
+                read_back(g)
+                load_next(2 * g + 1)
+            load_tokens(x_sb, x, 6, B)
+            unload_tokens(kT[0][:], flip_tokens(ps_head, k_sb[:, 0:NBLK, :]))
+
+        ps_flip = ctx.enter_context(tc.psum_pool(name="ps_flip", bufs=3, reuse_waits="tile"))
+        ps_score = ctx.enter_context(tc.psum_pool(name="ps_score", bufs=2, reuse_waits="tile"))
+        ps_eT = ctx.enter_context(tc.psum_pool(name="ps_eT", bufs=1, reuse_waits="tile"))
+        ps_mx = ctx.enter_context(tc.psum_pool(name="ps_mx", bufs=1, reuse_waits="tile"))
+
+        wv_grouped = keep.tile([P, H * PACK], BF16, align_bytes=64)
+        unload_features(
+            wv_grouped[:].bitcast(F32).rearrange("p (g r u) -> p g r u", g=1, u=2),
+            flip_features(wv_sb[:].bitcast(F32).rearrange("p (g w) -> p g w", g=1), 1),
+        )
+        wv_words, wv_scales = quantise(wv_grouped[:], keep, H, "wv")
+
+        for n in range(-1, B + 1):
+            step(n)

@@ -26,8 +26,12 @@ BANKS = ((3,), (2, 0), (1,))
 COL0 = {3: 0, 2: 512, 0: 896, 1: 1024}
 ROW = 1280
 PAD = 8
-GROUPS = ((0, 1), (2, 3, 4), (5, 6, 7))
-assert P * (3 * ROW + PAD) <= B * L * H
+PITCH = ROW + PAD
+SLOT = P * PITCH
+N_SLOTS = 3
+assert N_SLOTS * SLOT <= B * L * H
+
+Q_LOADS = ((0, 1), (1, N_SLOTS), (N_SLOTS, B))
 
 MASKED = -1.0e30
 SCALE = 1.0 / math.sqrt(H)
@@ -57,7 +61,7 @@ def tile_relativeattentionhead_pa_kernel(tc, x, q, k, Wv, rel_emb, out):
         relT = keep.tile([P, L], BF16)
         qT = [keep.tile([P, L], BF16, name="qT%d" % b) for b in range(B)]
         kT = [keep.tile([P, L], BF16, name="kT%d" % b) for b in range(B)]
-        m_rows = [keep.tile([P, len(GROUPS[g]) * ROW + PAD], F32, name="m_rows%d" % g) for g in range(len(GROUPS))]
+        m_rows = [keep.tile([P, PITCH], F32, name="m_rows%d" % b) for b in range(B)]
         s_sb = [keep.tile([P, ROW], F32, name="s_sb%d" % b) for b in range(B)]
         e_grouped = keep.tile([P, NBLK * P * PACK], BF16, align_bytes=64)
         out_sb = keep.tile([P, B * NBLK, H], F32)
@@ -75,7 +79,7 @@ def tile_relativeattentionhead_pa_kernel(tc, x, q, k, Wv, rel_emb, out):
         )
         make_identity(nc, ident_f32[:])
         for rows in m_rows:
-            nc.vector.memset(rows[:, rows.shape[1] - PAD :], 0.0)
+            nc.vector.memset(rows[:, ROW:PITCH], 0.0)
         nc.vector.memset(e_grouped[:], 0.0)
         nc.vector.tensor_copy(out=mask_bf[:], in_=mask_f32[:])
 
@@ -106,8 +110,8 @@ def tile_relativeattentionhead_pa_kernel(tc, x, q, k, Wv, rel_emb, out):
         def unload_tokens(dst, flipped):
             nc.vector.tensor_copy(out=dst, in_=flipped[:].rearrange("p g r -> p (g r)"))
 
-        def flip_features(src_words, n_groups):
-            flipped = ps_flip.tile([P, n_groups, 2, P], F32, tag="flip")
+        def flip_features(pool, src_words, n_groups):
+            flipped = pool.tile([P, n_groups, 2, P], F32, tag="flip")
             for g in range(n_groups):
                 for u in range(2):
                     nc.tensor.transpose(flipped[:, g, u, :], src_words[:, g, u * P : (u + 1) * P], ident_f32[:])
@@ -116,8 +120,7 @@ def tile_relativeattentionhead_pa_kernel(tc, x, q, k, Wv, rel_emb, out):
         def unload_features(dst_words, flipped):
             nc.scalar.copy(out=dst_words, in_=flipped[:].rearrange("p g u r -> p g r u"))
 
-        def rel_products(pool, g, j):
-            b = GROUPS[g][j]
+        def make_rows(pool, b):
             for bank, blocks in enumerate(BANKS):
                 first = COL0[blocks[0]]
                 m_ps = pool.tile([P, BANK], F32, tag="flip")
@@ -131,27 +134,16 @@ def tile_relativeattentionhead_pa_kernel(tc, x, q, k, Wv, rel_emb, out):
                         stop=True,
                     )
                 width = sum(WIDTH[blk] for blk in blocks)
-                copy_out(
-                    bank,
-                    m_rows[g][:, j * ROW + first : j * ROW + first + width],
-                    m_ps[:, 0:width],
-                )
+                copy_out(bank, m_rows[b][:, first : first + width], m_ps[:, 0:width])
 
-        def make_rows(pool, g):
-            for b in GROUPS[g]:
-                unload_tokens(qT[b][:], flip_tokens(pool, q_sb[:, b * NBLK : (b + 1) * NBLK, :]))
-            for j in range(len(GROUPS[g])):
-                rel_products(pool, g, j)
+        def store_rows(b):
+            base = (b % N_SLOTS) * SLOT
+            nc.sync.dma_start(out=out_flat[base : base + SLOT].rearrange("(p c) -> p c", c=PITCH), in_=m_rows[b][:])
 
-        def store_rows(g):
-            pitch = len(GROUPS[g]) * ROW + PAD
-            nc.sync.dma_start(out=out_flat[0 : P * pitch].rearrange("(p c) -> p c", c=pitch), in_=m_rows[g][:])
-
-        def read_back(g):
-            pitch = len(GROUPS[g]) * ROW + PAD
-            shifted = out_flat[P - 1 : P - 1 + P * (pitch - 1)].rearrange("(p c) -> p c", c=pitch - 1)
-            for j, b in enumerate(GROUPS[g]):
-                nc.sync.dma_start(out=s_sb[b][:], in_=shifted[:, j * ROW : (j + 1) * ROW])
+        def read_back(b):
+            base = (b % N_SLOTS) * SLOT + P - 1
+            shifted = out_flat[base : base + P * (PITCH - 1)].rearrange("(p c) -> p c", c=PITCH - 1)
+            nc.sync.dma_start(out=s_sb[b][:], in_=shifted[:, 0:ROW])
 
         x_flipped = {}
         x_mx = {}
@@ -167,14 +159,14 @@ def tile_relativeattentionhead_pa_kernel(tc, x, q, k, Wv, rel_emb, out):
 
         def flip_x(b):
             src = x_sb[:].bitcast(F32)[:, b * NBLK : (b + 1) * NBLK, :]
-            x_flipped[b] = [flip_features(src[:, 2 * half : 2 * half + 2, :], 2) for half in range(2)]
+            x_flipped[b] = [flip_features(ps_flip, src[:, 2 * half : 2 * half + 2, :], 2) for half in range(2)]
 
         def unload_x(b):
-            x_grouped = work.tile([P, L * PACK], BF16, align_bytes=64)
-            dst = x_grouped[:].bitcast(F32).rearrange("p (g r u) -> p g r u", g=NBLK, u=2)
+            grouped = work.tile([P, L * PACK], BF16, name="x_grouped", align_bytes=64)
+            dst = grouped[:].bitcast(F32).rearrange("p (g r u) -> p g r u", g=NBLK, u=2)
             for half in range(2):
                 unload_features(dst[:, 2 * half : 2 * half + 2], x_flipped[b][half])
-            return x_grouped
+            return grouped
 
         def project(b):
             v_ps[b] = ps_mx.tile([P, NBLK, H], F32, name="v_ps", tag="mx")
@@ -352,37 +344,44 @@ def tile_relativeattentionhead_pa_kernel(tc, x, q, k, Wv, rel_emb, out):
                 project(n)
 
         nc.sync.dma_start(out=rel_sb[:], in_=rel_emb.rearrange("(g p) h -> p g h", p=P))
-        load_tokens(q_sb, q, 0, 2)
-        load_tokens(q_sb, q, 2, B)
+        for first, stop in Q_LOADS:
+            load_tokens(q_sb, q, first, stop)
         load_tokens(k_sb, k, 0, 2)
         nc.sync.dma_start(out=wv_sb[:], in_=Wv)
 
-        def load_next(i):
-            load_tokens(x_sb, x, i, i + 1)
-            load_tokens(k_sb, k, i + 2, i + 3)
-
         with tc.psum_pool(name="ps_head", bufs=8) as ps_head:
             unload_tokens(relT[:], flip_tokens(ps_head, rel_sb))
-            for g in range(len(GROUPS)):
-                make_rows(ps_head, g)
-                store_rows(g)
-                load_next(2 * g)
-                read_back(g)
-                load_next(2 * g + 1)
-            load_tokens(x_sb, x, 6, B)
-            unload_tokens(kT[0][:], flip_tokens(ps_head, k_sb[:, 0:NBLK, :]))
+            for first, stop in Q_LOADS:
+                for b in range(first, stop):
+                    unload_tokens(qT[b][:], flip_tokens(ps_head, q_sb[:, b * NBLK : (b + 1) * NBLK, :]))
+                for b in range(first, stop):
+                    make_rows(ps_head, b)
+            for b in range(2):
+                unload_tokens(kT[b][:], flip_tokens(ps_head, k_sb[:, b * NBLK : (b + 1) * NBLK, :]))
+            wv_grouped = keep.tile([P, H * PACK], BF16, align_bytes=64)
+            unload_features(
+                wv_grouped[:].bitcast(F32).rearrange("p (g r u) -> p g r u", g=1, u=2),
+                flip_features(ps_head, wv_sb[:].bitcast(F32).rearrange("p (g w) -> p g w", g=1), 1),
+            )
+            wv_words, wv_scales = quantise(wv_grouped[:], keep, H, "wv")
+
+        store_rows(0)
+        store_rows(1)
+        for b in range(B):
+            load_tokens(x_sb, x, b, b + 1)
+            if live(b + 2):
+                load_tokens(k_sb, k, b + 2, b + 3)
+            read_back(b)
+            if live(b + 2):
+                store_rows(b + 2)
 
         ps_flip = ctx.enter_context(tc.psum_pool(name="ps_flip", bufs=3, reuse_waits="tile"))
         ps_score = ctx.enter_context(tc.psum_pool(name="ps_score", bufs=2, reuse_waits="tile"))
         ps_eT = ctx.enter_context(tc.psum_pool(name="ps_eT", bufs=1, reuse_waits="tile"))
         ps_mx = ctx.enter_context(tc.psum_pool(name="ps_mx", bufs=1, reuse_waits="tile"))
 
-        wv_grouped = keep.tile([P, H * PACK], BF16, align_bytes=64)
-        unload_features(
-            wv_grouped[:].bitcast(F32).rearrange("p (g r u) -> p g r u", g=1, u=2),
-            flip_features(wv_sb[:].bitcast(F32).rearrange("p (g w) -> p g w", g=1), 1),
-        )
-        wv_words, wv_scales = quantise(wv_grouped[:], keep, H, "wv")
-
-        for n in range(-1, B + 1):
+        scores(0, 0)
+        scores(0, 1)
+        flip_x(0)
+        for n in range(B + 1):
             step(n)

@@ -253,10 +253,12 @@ def tile_relativeattentionhead_pa_kernel(tc, x, q, k, Wv, rel_emb, out):
                         accum_out=row_sum[b][:, blk : blk + 1],
                     )
                     for t in range(blk + 1):
-                        nc.tensor.transpose(
+                        nc.tensor.matmul(
                             eT_ps[b][blk % 2][:, first_plane(blk) + t, :],
-                            e_sb[b][:, COL0[blk] + t * P : COL0[blk] + (t + 1) * P],
-                            ident_bf[:],
+                            lhsT=e_sb[b][:, COL0[blk] + t * P : COL0[blk] + (t + 1) * P],
+                            rhs=ident_bf[:],
+                            start=True,
+                            stop=True,
                         )
 
         def first_plane(blk):

@@ -25,6 +25,9 @@ WIDTH = {0: 128, 1: 256, 2: 384, 3: 512}
 BANKS = ((3,), (2, 0), (1,))
 COL0 = {3: 0, 2: 512, 0: 896, 1: 1024}
 ROW = 1280
+E_COL0 = {3: 0, 2: 512, 1: 1024, 0: 1280}
+E_ROW = 1536
+E_BANKS = ((3, 2), (1, 0))
 PAD = 8
 PITCH = ROW + PAD
 SLOT = P * PITCH
@@ -64,6 +67,8 @@ def tile_relativeattentionhead_pa_kernel(tc, x, q, k, Wv, rel_emb, out):
         m_rows = [keep.tile([P, PITCH], F32, name="m_rows%d" % b) for b in range(B)]
         s_sb = [keep.tile([P, ROW], F32, name="s_sb%d" % b) for b in range(B)]
         e_grouped = keep.tile([P, NBLK * P * PACK], BF16, align_bytes=64)
+        e_sbs = [keep.tile([P, E_ROW], BF16, name="e_sb%d" % i) for i in range(2)]
+        zero_f32 = keep.tile([P, P], F32)
         out_sb = keep.tile([P, B * NBLK, H], F32)
 
         make_identity(nc, ident_bf[:])
@@ -80,7 +85,10 @@ def tile_relativeattentionhead_pa_kernel(tc, x, q, k, Wv, rel_emb, out):
         make_identity(nc, ident_f32[:])
         for rows in m_rows:
             nc.vector.memset(rows[:, ROW:PITCH], 0.0)
-        nc.vector.memset(e_grouped[:], 0.0)
+        nc.vector.memset(zero_f32[:], 0.0)
+        for es in e_sbs:
+            for blk in (2, 0):
+                nc.vector.memset(es[:, E_COL0[blk] + WIDTH[blk] : E_COL0[blk] + WIDTH[blk] + P], 0.0)
         nc.vector.tensor_copy(out=mask_bf[:], in_=mask_f32[:])
 
         def load_tokens(dst, src, first, stop):
@@ -106,6 +114,12 @@ def tile_relativeattentionhead_pa_kernel(tc, x, q, k, Wv, rel_emb, out):
             for g in range(NBLK):
                 nc.tensor.transpose(flipped[:, g, :], src[:, g, :], ident_bf[:])
             return flipped
+
+        def load_x(b):
+            nc.sync.dma_start(
+                out=x_sb[:, b * NBLK : (b + 1) * NBLK, :].rearrange("p (u e) f -> p u (e f)", u=2),
+                in_=x[b].rearrange("(u p e) f -> p u (e f)", u=2, e=2),
+            )
 
         def unload_tokens(dst, flipped):
             nc.vector.tensor_copy(out=dst, in_=flipped[:].rearrange("p g r -> p (g r)"))
@@ -151,7 +165,6 @@ def tile_relativeattentionhead_pa_kernel(tc, x, q, k, Wv, rel_emb, out):
         v_mx = {}
         qk_ps = {}
         e_sb = {}
-        eT_ps = {}
         e_mx = {}
         o_ps = {}
         neg_max = {}
@@ -235,44 +248,32 @@ def tile_relativeattentionhead_pa_kernel(tc, x, q, k, Wv, rel_emb, out):
                 )
 
         def exponentiate(b):
-            e_sb[b] = work.tile([P, ROW], BF16, name="e_sb")
+            e_sb[b] = e_sbs[b % 2]
+            e_words = e_sb[b][:].bitcast(F32)
             row_sum[b] = small.tile([P, NBLK], F32, name="row_sum")
-            eT_ps[b] = [
-                ps_eT.tile([P, 4, P], BF16, name="eT_even"),
-                ps_eT.tile([P, 6, P], BF16, name="eT_odd"),
-            ]
             for blocks in BANKS:
                 for blk in blocks:
                     cols = slice(COL0[blk], COL0[blk] + WIDTH[blk])
                     nc.scalar.activation(
-                        out=e_sb[b][:, cols],
+                        out=e_sb[b][:, E_COL0[blk] : E_COL0[blk] + WIDTH[blk]],
                         in_=s_sb[b][:, cols],
                         func=ACT.Exp,
                         bias=neg_max[b][:, blk : blk + 1],
                         scale=1.0,
                         accum_out=row_sum[b][:, blk : blk + 1],
                     )
-                    for t in range(blk + 1):
-                        nc.tensor.matmul(
-                            eT_ps[b][blk % 2][:, first_plane(blk) + t, :],
-                            lhsT=e_sb[b][:, COL0[blk] + t * P : COL0[blk] + (t + 1) * P],
-                            rhs=ident_bf[:],
-                            start=True,
-                            stop=True,
-                        )
+                    for u in range(1 + blk // 2):
+                        first = E_COL0[blk] // 2 + u * P
+                        nc.tensor.transpose(eT_plane(blk, u), e_words[:, first : first + P], ident_f32[:])
 
-        def first_plane(blk):
-            return 0 if blk >= 2 else blk + 3
+        def eT_plane(blk, u):
+            bank = 0 if blk in E_BANKS[0] else 1
+            return eT_banks[bank][:, E_BANKS[bank].index(blk), u, :]
 
         def unload_e(b):
-            for blocks in BANKS:
-                for blk in blocks:
-                    places = e_grouped[:, blk * P * PACK : (blk + 1) * P * PACK]
-                    planes = eT_ps[b][blk % 2][:, first_plane(blk) : first_plane(blk) + blk + 1, :]
-                    nc.scalar.copy(
-                        out=places.rearrange("p (i t) -> p i t", t=PACK)[:, :, 0 : blk + 1],
-                        in_=planes.rearrange("p t i -> p i t"),
-                    )
+            words = e_grouped[:].bitcast(F32).rearrange("p (k g i u) -> p k g i u", k=2, g=2, u=2)
+            for bank in range(len(E_BANKS)):
+                nc.scalar.copy(out=words[:, bank], in_=eT_banks[bank][:].rearrange("p g u i -> p g i u"))
 
         def weighted_sum(b):
             o_ps[b] = ps_mx.tile([P, NBLK, H], F32, name="o_ps", tag="mx")
@@ -281,8 +282,8 @@ def tile_relativeattentionhead_pa_kernel(tc, x, q, k, Wv, rel_emb, out):
             for blk in range(NBLK):
                 nc.tensor.matmul_mx(
                     out=o_ps[b][:, blk, :],
-                    lhsT=e_words[:, blk * P : (blk + 1) * P].bitcast(FP8X4),
-                    lhsT_scale=e_scales[:, blk * P : (blk + 1) * P],
+                    lhsT=e_words[:, (3 - blk) * P : (4 - blk) * P].bitcast(FP8X4),
+                    lhsT_scale=e_scales[:, (3 - blk) * P : (4 - blk) * P],
                     rhs=v_words[:].bitcast(FP8X4),
                     rhs_scale=v_scales[:],
                     start=True,
@@ -370,7 +371,7 @@ def tile_relativeattentionhead_pa_kernel(tc, x, q, k, Wv, rel_emb, out):
         store_rows(0)
         store_rows(1)
         for b in range(B):
-            load_tokens(x_sb, x, b, b + 1)
+            load_x(b)
             if live(b + 2):
                 load_tokens(k_sb, k, b + 2, b + 3)
             read_back(b)
@@ -381,6 +382,9 @@ def tile_relativeattentionhead_pa_kernel(tc, x, q, k, Wv, rel_emb, out):
         ps_score = ctx.enter_context(tc.psum_pool(name="ps_score", bufs=2, reuse_waits="tile"))
         ps_eT = ctx.enter_context(tc.psum_pool(name="ps_eT", bufs=1, reuse_waits="tile"))
         ps_mx = ctx.enter_context(tc.psum_pool(name="ps_mx", bufs=1, reuse_waits="tile"))
+        eT_banks = [ps_eT.tile([P, 2, 2, P], F32, name="eT_bank%d" % i) for i in range(2)]
+        for g in range(2):
+            nc.tensor.transpose(eT_banks[1][:, g, 1, :], zero_f32[:], ident_f32[:])
 
         scores(0, 0)
         scores(0, 1)

@@ -52,6 +52,7 @@ def tile_relativeattentionhead_pa_kernel(tc, x, q, k, Wv, rel_emb, out):
         small = ctx.enter_context(tc.tile_pool(name="small", bufs=4))
         ctx.enter_context(tc.manual_schedule())
 
+        idle_bf = keep.tile([P, BANK], BF16)
         ident_bf = keep.tile([P, P], BF16)
         ident_f32 = keep.tile([P, P], F32)
         mask_f32 = keep.tile([P, P], F32)
@@ -71,6 +72,7 @@ def tile_relativeattentionhead_pa_kernel(tc, x, q, k, Wv, rel_emb, out):
         zero_f32 = keep.tile([P, P], F32)
         out_sb = keep.tile([P, B * NBLK, H], F32)
 
+        nc.vector.memset(idle_bf[:], 0.0)
         make_identity(nc, ident_bf[:])
         nc.gpsimd.memset(mask_f32[:], 0.0)
         nc.gpsimd.affine_select(
@@ -124,8 +126,14 @@ def tile_relativeattentionhead_pa_kernel(tc, x, q, k, Wv, rel_emb, out):
         def unload_tokens(dst, flipped):
             nc.vector.tensor_copy(out=dst, in_=flipped[:].rearrange("p g r -> p (g r)"))
 
-        def flip_features(pool, src_words, n_groups):
+        def keep_warm(tile, times):
+            for i in range(times):
+                nc.tensor.matmul(tile, lhsT=idle_bf[:, 0:P], rhs=idle_bf[:], start=True, stop=True)
+
+        def flip_features(pool, src_words, n_groups, warm=0):
             flipped = pool.tile([P, n_groups, 2, P], F32, tag="flip")
+            if warm:
+                keep_warm(flipped[:].rearrange("p g u r -> p (g u r)"), warm)
             for g in range(n_groups):
                 for u in range(2):
                     nc.tensor.transpose(flipped[:, g, u, :], src_words[:, g, u * P : (u + 1) * P], ident_f32[:])
@@ -169,10 +177,11 @@ def tile_relativeattentionhead_pa_kernel(tc, x, q, k, Wv, rel_emb, out):
         o_ps = {}
         neg_max = {}
         row_sum = {}
+        inv_sum = {}
 
         def flip_x(b):
             src = x_sb[:].bitcast(F32)[:, b * NBLK : (b + 1) * NBLK, :]
-            x_flipped[b] = [flip_features(ps_flip, src[:, 2 * half : 2 * half + 2, :], 2) for half in range(2)]
+            x_flipped[b] = [flip_features(ps_flip, src[:, 2 * half : 2 * half + 2, :], 2, 1 - half) for half in range(2)]
 
         def unload_x(b):
             grouped = work.tile([P, L * PACK], BF16, name="x_grouped", align_bytes=64)
@@ -279,6 +288,7 @@ def tile_relativeattentionhead_pa_kernel(tc, x, q, k, Wv, rel_emb, out):
             o_ps[b] = ps_mx.tile([P, NBLK, H], F32, name="o_ps", tag="mx")
             e_words, e_scales = e_mx[b]
             v_words, v_scales = v_mx[b]
+            keep_warm(o_ps[b][:].rearrange("p t h -> p (t h)"), 1)
             for blk in range(NBLK):
                 nc.tensor.matmul_mx(
                     out=o_ps[b][:, blk, :],
@@ -290,13 +300,15 @@ def tile_relativeattentionhead_pa_kernel(tc, x, q, k, Wv, rel_emb, out):
                     stop=True,
                 )
 
+        def invert_sums(b):
+            inv_sum[b] = small.tile([P, NBLK], F32, name="inv_sum")
+            nc.vector.reciprocal(out=inv_sum[b][:], in_=row_sum[b][:])
+
         def normalise(b):
-            inv_sum = small.tile([P, NBLK], F32)
-            nc.vector.reciprocal(out=inv_sum[:], in_=row_sum[b][:])
             nc.vector.tensor_tensor(
                 out=out_sb[:, b * NBLK : (b + 1) * NBLK, :],
                 in0=o_ps[b][:],
-                in1=inv_sum[:].unsqueeze(2).to_broadcast([P, NBLK, H]),
+                in1=inv_sum[b][:].unsqueeze(2).to_broadcast([P, NBLK, H]),
                 op=ALU.mult,
             )
 
@@ -326,13 +338,15 @@ def tile_relativeattentionhead_pa_kernel(tc, x, q, k, Wv, rel_emb, out):
             if live(n - 1):
                 e_mx[n - 1] = quantise(e_grouped[:], work, L, "e")
                 v_mx[n - 1] = quantise(v_grouped[:], work, H, "v")
+                invert_sums(n - 1)
                 weighted_sum(n - 1)
             if live(n):
                 row_max(n, len(BANKS) - 1)
                 x_grouped = unload_x(n)
-                exponentiate(n)
             if live(n + 1):
                 flip_x(n + 1)
+            if live(n):
+                exponentiate(n)
             if live(n + 2):
                 unload_tokens(kT[n + 2][:], k_flipped)
             if live(n):
@@ -353,6 +367,7 @@ def tile_relativeattentionhead_pa_kernel(tc, x, q, k, Wv, rel_emb, out):
         nc.sync.dma_start(out=wv_sb[:], in_=Wv)
 
         with tc.psum_pool(name="ps_head", bufs=8) as ps_head:
+            keep_warm(ps_head.tile([P, BANK], F32, name="warm", tag="flip")[:], 5)
             unload_tokens(relT[:], flip_tokens(ps_head, rel_sb))
             for first, stop in Q_LOADS:
                 for b in range(first, stop):

@@ -191,7 +191,10 @@ def tile_relativeattentionhead_pa_kernel(tc, x, q, k, Wv, rel_emb, out):
             return grouped
 
         def project(b):
-            v_ps[b] = ps_mx.tile([P, NBLK, H], F32, name="v_ps", tag="mx")
+            if b < B - 1:
+                v_ps[b] = ps_mx.tile([P, NBLK, H], F32, name="v_ps", tag="mx")
+            else:
+                v_ps[b] = ps_score.tile([P, NBLK, H], F32, name="v_ps", tag="score")
             x_words, x_scales = x_mx[b]
             for t in range(NBLK):
                 nc.tensor.matmul_mx(
@@ -205,7 +208,7 @@ def tile_relativeattentionhead_pa_kernel(tc, x, q, k, Wv, rel_emb, out):
                 )
 
         def unload_v(b):
-            v_grouped = work.tile([P, H * PACK], BF16, align_bytes=64)
+            v_grouped = work.tile([P, H * PACK], BF16, name="v_grouped", align_bytes=64)
             nc.scalar.copy(
                 out=v_grouped[:].rearrange("p (h t) -> p h t", t=PACK),
                 in_=v_ps[b][:].rearrange("p t h -> p h t"),
@@ -279,16 +282,49 @@ def tile_relativeattentionhead_pa_kernel(tc, x, q, k, Wv, rel_emb, out):
             bank = 0 if blk in E_BANKS[0] else 1
             return eT_banks[bank][:, E_BANKS[bank].index(blk), u, :]
 
-        def unload_e(b):
+        def unload_e(b, banks=(0, 1)):
             words = e_grouped[:].bitcast(F32).rearrange("p (k g i u) -> p k g i u", k=2, g=2, u=2)
-            for bank in range(len(E_BANKS)):
+            for bank in banks:
                 nc.scalar.copy(out=words[:, bank], in_=eT_banks[bank][:].rearrange("p g u i -> p g i u"))
+
+        def finish_last():
+            b = B - 1
+            v_words, v_scales = v_mx[b]
+            halves = [quantise(e_grouped[:, i * 2 * P * PACK : (i + 1) * 2 * P * PACK], work, 2 * P, "e_half") for i in range(2)]
+            normalise(b - 1)
+            store(b - 1, b)
+            o_half = []
+            for bank, pool, tag in ((0, ps_score, "score"), (1, ps_flip, "flip")):
+                e_words, e_scales = halves[bank]
+                o = pool.tile([P, 2, H], F32, name="o_half", tag=tag)
+                for i in range(2):
+                    nc.tensor.matmul_mx(
+                        out=o[:, 1 - i, :],
+                        lhsT=e_words[:, i * P : (i + 1) * P].bitcast(FP8X4),
+                        lhsT_scale=e_scales[:, i * P : (i + 1) * P],
+                        rhs=v_words[:].bitcast(FP8X4),
+                        rhs_scale=v_scales[:],
+                        start=True,
+                        stop=True,
+                    )
+                first = 2 * (1 - bank)
+                nc.vector.tensor_tensor(
+                    out=out_sb[:, b * NBLK + first : b * NBLK + first + 2, :],
+                    in0=o[:],
+                    in1=inv_sum[b][:, first : first + 2].unsqueeze(2).to_broadcast([P, 2, H]),
+                    op=ALU.mult,
+                )
+                nc.sync.dma_start(
+                    out=out[b, first * P : (first + 2) * P].rearrange("(g p) h -> p g h", p=P),
+                    in_=out_sb[:, b * NBLK + first : b * NBLK + first + 2, :],
+                )
 
         def weighted_sum(b):
             o_ps[b] = ps_mx.tile([P, NBLK, H], F32, name="o_ps", tag="mx")
             e_words, e_scales = e_mx[b]
             v_words, v_scales = v_mx[b]
-            keep_warm(o_ps[b][:].rearrange("p t h -> p (t h)"), 1)
+            if b < B - 2:
+                keep_warm(o_ps[b][:].rearrange("p t h -> p (t h)"), 1)
             for blk in range(NBLK):
                 nc.tensor.matmul_mx(
                     out=o_ps[b][:, blk, :],
@@ -322,6 +358,8 @@ def tile_relativeattentionhead_pa_kernel(tc, x, q, k, Wv, rel_emb, out):
             return 0 <= b < B
 
         def step(n):
+            if live(n):
+                x_grouped = unload_x(n)
             if live(n - 1):
                 unload_e(n - 1)
                 v_grouped = unload_v(n - 1)
@@ -338,20 +376,18 @@ def tile_relativeattentionhead_pa_kernel(tc, x, q, k, Wv, rel_emb, out):
             if live(n - 1):
                 e_mx[n - 1] = quantise(e_grouped[:], work, L, "e")
                 v_mx[n - 1] = quantise(v_grouped[:], work, H, "v")
-                invert_sums(n - 1)
                 weighted_sum(n - 1)
             if live(n):
                 row_max(n, len(BANKS) - 1)
-                x_grouped = unload_x(n)
+                x_mx[n] = quantise(x_grouped[:], work, L, "x")
             if live(n + 1):
                 flip_x(n + 1)
             if live(n):
                 exponentiate(n)
             if live(n + 2):
-                unload_tokens(kT[n + 2][:], k_flipped)
-            if live(n):
-                x_mx[n] = quantise(x_grouped[:], work, L, "x")
+                nc.scalar.copy(out=kT[n + 2][:], in_=k_flipped[:].rearrange("p g r -> p (g r)"))
             if live(n - 1):
+                invert_sums(n - 1)
                 normalise(n - 1)
                 if n - 1 == FIRST_STORE:
                     store(0, n)
@@ -359,6 +395,35 @@ def tile_relativeattentionhead_pa_kernel(tc, x, q, k, Wv, rel_emb, out):
                     store(n - 1, n)
             if live(n):
                 project(n)
+
+        def last_step():
+            n = B - 1
+            x_grouped = unload_x(n)
+            unload_e(n - 1)
+            v_grouped = unload_v(n - 1)
+            for bank in range(len(BANKS)):
+                add_rel(n, bank)
+                if bank > 0:
+                    row_max(n, bank - 1)
+                if bank == 0:
+                    scores(n, 2)
+                if bank == 1:
+                    x_mx[n] = quantise(x_grouped[:], work, L, "x")
+            row_max(n, len(BANKS) - 1)
+            project(n)
+            e_mx[n - 1] = quantise(e_grouped[:], work, L, "e")
+            v_mx[n - 1] = quantise(v_grouped[:], work, H, "v")
+            exponentiate(n)
+            invert_sums(n - 1)
+            v_last = work.tile([P, H * PACK], BF16, name="v_grouped", align_bytes=64)
+            nc.vector.tensor_copy(out=v_last[:].rearrange("p (h t) -> p h t", t=PACK), in_=v_ps[n][:].rearrange("p t h -> p h t"))
+            weighted_sum(n - 1)
+            unload_e(n, (0,))
+            unload_e(n, (1,))
+            v_mx[n] = quantise(v_last[:], work, H, "v")
+            invert_sums(n)
+            finish_last()
+
 
         nc.sync.dma_start(out=rel_sb[:], in_=rel_emb.rearrange("(g p) h -> p g h", p=P))
         for first, stop in Q_LOADS:
@@ -404,5 +469,6 @@ def tile_relativeattentionhead_pa_kernel(tc, x, q, k, Wv, rel_emb, out):
         scores(0, 0)
         scores(0, 1)
         flip_x(0)
-        for n in range(B + 1):
+        for n in range(B - 1):
             step(n)
+        last_step()

@@ -93,6 +93,12 @@ def tile_relativeattentionhead_pa_kernel(tc, x, q, k, Wv, rel_emb, out):
                 nc.vector.memset(es[:, E_COL0[blk] + WIDTH[blk] : E_COL0[blk] + WIDTH[blk] + P], 0.0)
         nc.vector.tensor_copy(out=mask_bf[:], in_=mask_f32[:])
 
+        def load_rows(dst, src, first, stop):
+            nc.sync.dma_start(
+                out=dst[:, first * NBLK : stop * NBLK, :].rearrange("p (b g) f -> p b (g f)", g=NBLK),
+                in_=src[first:stop].rearrange("b (p g) f -> p b (g f)", p=P),
+            )
+
         def load_tokens(dst, src, first, stop):
             nc.sync.dma_start(
                 out=dst[:, first * NBLK : stop * NBLK, :],
@@ -171,6 +177,7 @@ def tile_relativeattentionhead_pa_kernel(tc, x, q, k, Wv, rel_emb, out):
         x_mx = {}
         v_ps = {}
         v_mx = {}
+        x_grouped = {}
         qk_ps = {}
         e_sb = {}
         e_mx = {}
@@ -181,7 +188,7 @@ def tile_relativeattentionhead_pa_kernel(tc, x, q, k, Wv, rel_emb, out):
 
         def flip_x(b):
             src = x_sb[:].bitcast(F32)[:, b * NBLK : (b + 1) * NBLK, :]
-            x_flipped[b] = [flip_features(ps_flip, src[:, 2 * half : 2 * half + 2, :], 2, 1 - half) for half in range(2)]
+            x_flipped[b] = [flip_features(ps_flip, src[:, 2 * half : 2 * half + 2, :], 2, 0) for half in range(2)]
 
         def unload_x(b):
             grouped = work.tile([P, L * PACK], BF16, name="x_grouped", align_bytes=64)
@@ -323,8 +330,6 @@ def tile_relativeattentionhead_pa_kernel(tc, x, q, k, Wv, rel_emb, out):
             o_ps[b] = ps_mx.tile([P, NBLK, H], F32, name="o_ps", tag="mx")
             e_words, e_scales = e_mx[b]
             v_words, v_scales = v_mx[b]
-            if b < B - 2:
-                keep_warm(o_ps[b][:].rearrange("p t h -> p (t h)"), 1)
             for blk in range(NBLK):
                 nc.tensor.matmul_mx(
                     out=o_ps[b][:, blk, :],
@@ -359,57 +364,63 @@ def tile_relativeattentionhead_pa_kernel(tc, x, q, k, Wv, rel_emb, out):
 
         def step(n):
             if live(n):
-                x_grouped = unload_x(n)
+                x_grouped[n] = unload_x(n)
             if live(n - 1):
                 unload_e(n - 1)
-                v_grouped = unload_v(n - 1)
-            for bank in range(len(BANKS)):
-                if live(n):
-                    add_rel(n, bank)
-                    if bank > 0:
-                        row_max(n, bank - 1)
-                ahead = bank + 2
-                if live(n + ahead // len(BANKS)):
-                    scores(n + ahead // len(BANKS), ahead % len(BANKS))
+            add_rel(n, 0)
+            scores(n, 2)
             if live(n + 2):
                 k_flipped = flip_tokens(ps_flip, k_sb[:, (n + 2) * NBLK : (n + 3) * NBLK, :])
+            if live(n - 2):
+                normalise(n - 2)
+                store_results(n - 2)
+            if live(n - 1):
+                project(n - 1)
+                v_grouped = unload_v(n - 1)
+            add_rel(n, 1)
+            if live(n + 1):
+                scores(n + 1, 0)
+            row_max(n, 0)
+            add_rel(n, 2)
+            if live(n + 1):
+                scores(n + 1, 1)
+            row_max(n, 1)
+            row_max(n, 2)
+            if live(n + 1):
+                flip_x(n + 1)
             if live(n - 1):
                 e_mx[n - 1] = quantise(e_grouped[:], work, L, "e")
                 v_mx[n - 1] = quantise(v_grouped[:], work, H, "v")
                 weighted_sum(n - 1)
-            if live(n):
-                row_max(n, len(BANKS) - 1)
-                x_mx[n] = quantise(x_grouped[:], work, L, "x")
-            if live(n + 1):
-                flip_x(n + 1)
-            if live(n):
-                exponentiate(n)
+            x_mx[n] = quantise(x_grouped[n][:], work, L, "x")
+            exponentiate(n)
             if live(n + 2):
-                nc.scalar.copy(out=kT[n + 2][:], in_=k_flipped[:].rearrange("p g r -> p (g r)"))
+                nc.scalar.copy(out=kT[n + 2][:].rearrange("p (r g) -> p r g", g=NBLK), in_=k_flipped[:].rearrange("p g r -> p r g"))
             if live(n - 1):
                 invert_sums(n - 1)
-                normalise(n - 1)
-                if n - 1 == FIRST_STORE:
-                    store(0, n)
-                elif n - 1 > FIRST_STORE:
-                    store(n - 1, n)
-            if live(n):
-                project(n)
+
+        def store_results(b):
+            if b == FIRST_STORE:
+                store(0, b + 1)
+            elif b > FIRST_STORE:
+                store(b, b + 1)
 
         def last_step():
             n = B - 1
-            x_grouped = unload_x(n)
+            x_grouped[n] = unload_x(n)
             unload_e(n - 1)
+            add_rel(n, 0)
+            scores(n, 2)
+            normalise(n - 2)
+            store_results(n - 2)
+            project(n - 1)
             v_grouped = unload_v(n - 1)
-            for bank in range(len(BANKS)):
-                add_rel(n, bank)
-                if bank > 0:
-                    row_max(n, bank - 1)
-                if bank == 0:
-                    scores(n, 2)
-                if bank == 1:
-                    x_mx[n] = quantise(x_grouped[:], work, L, "x")
-            row_max(n, len(BANKS) - 1)
+            add_rel(n, 1)
+            row_max(n, 0)
+            x_mx[n] = quantise(x_grouped[n][:], work, L, "x")
+            add_rel(n, 2)
+            row_max(n, 1)
+            row_max(n, 2)
             project(n)
             e_mx[n - 1] = quantise(e_grouped[:], work, L, "e")
             v_mx[n - 1] = quantise(v_grouped[:], work, H, "v")
@@ -428,7 +439,7 @@ def tile_relativeattentionhead_pa_kernel(tc, x, q, k, Wv, rel_emb, out):
         nc.sync.dma_start(out=rel_sb[:], in_=rel_emb.rearrange("(g p) h -> p g h", p=P))
         for first, stop in Q_LOADS:
             load_tokens(q_sb, q, first, stop)
-        load_tokens(k_sb, k, 0, 2)
+        load_rows(k_sb, k, 0, 2)
         nc.sync.dma_start(out=wv_sb[:], in_=Wv)
 
         with tc.psum_pool(name="ps_head", bufs=8) as ps_head:
@@ -440,7 +451,7 @@ def tile_relativeattentionhead_pa_kernel(tc, x, q, k, Wv, rel_emb, out):
                 for b in range(first, stop):
                     make_rows(ps_head, b)
             for b in range(2):
-                unload_tokens(kT[b][:], flip_tokens(ps_head, k_sb[:, b * NBLK : (b + 1) * NBLK, :]))
+                nc.vector.tensor_copy(out=kT[b][:].rearrange("p (r g) -> p r g", g=NBLK), in_=flip_tokens(ps_head, k_sb[:, b * NBLK : (b + 1) * NBLK, :])[:].rearrange("p g r -> p r g"))
             wv_grouped = keep.tile([P, H * PACK], BF16, align_bytes=64)
             unload_features(
                 wv_grouped[:].bitcast(F32).rearrange("p (g r u) -> p g r u", g=1, u=2),
@@ -448,15 +459,22 @@ def tile_relativeattentionhead_pa_kernel(tc, x, q, k, Wv, rel_emb, out):
             )
             wv_words, wv_scales = quantise(wv_grouped[:], keep, H, "wv")
 
+        load_x(0)
         store_rows(0)
         store_rows(1)
-        for b in range(B):
+        load_rows(k_sb, k, 2, 3)
+        read_back(0)
+        load_x(1)
+        store_rows(2)
+        load_rows(k_sb, k, 3, 4)
+        read_back(1)
+        for b in range(2, B):
+            if live(b + 1):
+                store_rows(b + 1)
             load_x(b)
             if live(b + 2):
-                load_tokens(k_sb, k, b + 2, b + 3)
+                load_rows(k_sb, k, b + 2, b + 3)
             read_back(b)
-            if live(b + 2):
-                store_rows(b + 2)
 
         ps_flip = ctx.enter_context(tc.psum_pool(name="ps_flip", bufs=3, reuse_waits="tile"))
         ps_score = ctx.enter_context(tc.psum_pool(name="ps_score", bufs=2, reuse_waits="tile"))

@@ -34,7 +34,7 @@ SLOT = P * PITCH
 N_SLOTS = 3
 assert N_SLOTS * SLOT <= B * L * H
 
-Q_LOADS = ((0, 1), (1, N_SLOTS), (N_SLOTS, B))
+Q_LOADS = ((0, 1), (1, 3), (3, 5), (5, B))
 
 MASKED = -1.0e30
 SCALE = 1.0 / math.sqrt(H)
@@ -229,17 +229,9 @@ def tile_relativeattentionhead_pa_kernel(tc, x, q, k, Wv, rel_emb, out):
             for blk in blocks:
                 lo = COL0[blk] - first
                 queries = qT[b][:, blk * P : (blk + 1) * P]
-                if blk > 0:
-                    nc.tensor.matmul(
-                        qk_ps[b, bank][:, lo : lo + blk * P],
-                        lhsT=queries,
-                        rhs=kT[b][:, 0 : blk * P],
-                        start=True,
-                        stop=True,
-                    )
-                diagonal = qk_ps[b, bank][:, lo + blk * P : lo + (blk + 1) * P]
-                nc.tensor.matmul(diagonal, lhsT=queries, rhs=kT[b][:, blk * P : (blk + 1) * P], start=True, stop=False)
-                nc.tensor.matmul(diagonal, lhsT=ident_bf[:], rhs=mask_bf[:], start=False, stop=True)
+                out = qk_ps[b, bank][:, lo : lo + WIDTH[blk]]
+                nc.tensor.matmul(out, lhsT=queries, rhs=kT[b][:, 0 : WIDTH[blk]], start=True, stop=False)
+                nc.tensor.matmul(out[:, blk * P : WIDTH[blk]], lhsT=ident_bf[:], rhs=mask_bf[:], start=False, stop=True)
 
         def add_rel(b, bank):
             blocks = BANKS[bank]
@@ -298,7 +290,13 @@ def tile_relativeattentionhead_pa_kernel(tc, x, q, k, Wv, rel_emb, out):
             b = B - 1
             v_words, v_scales = v_mx[b]
             halves = [quantise(e_grouped[:, i * 2 * P * PACK : (i + 1) * 2 * P * PACK], work, 2 * P, "e_half") for i in range(2)]
-            normalise(b - 1)
+            for blk in range(NBLK):
+                nc.scalar.activation(
+                    out=out_sb[:, (b - 1) * NBLK + blk, :],
+                    in_=o_ps[b - 1][:, blk, :],
+                    func=ACT.Copy,
+                    scale=inv_sum[b - 1][:, blk : blk + 1],
+                )
             store(b - 1, b)
             o_half = []
             for bank, pool, tag in ((0, ps_score, "score"), (1, ps_flip, "flip")):
@@ -367,10 +365,10 @@ def tile_relativeattentionhead_pa_kernel(tc, x, q, k, Wv, rel_emb, out):
                 x_grouped[n] = unload_x(n)
             if live(n - 1):
                 unload_e(n - 1)
-            add_rel(n, 0)
-            scores(n, 2)
             if live(n + 2):
                 k_flipped = flip_tokens(ps_flip, k_sb[:, (n + 2) * NBLK : (n + 3) * NBLK, :])
+            add_rel(n, 0)
+            scores(n, 2)
             if live(n - 2):
                 normalise(n - 2)
                 store_results(n - 2)
@@ -380,14 +378,13 @@ def tile_relativeattentionhead_pa_kernel(tc, x, q, k, Wv, rel_emb, out):
             add_rel(n, 1)
             if live(n + 1):
                 scores(n + 1, 0)
+                flip_x(n + 1)
             row_max(n, 0)
             add_rel(n, 2)
             if live(n + 1):
                 scores(n + 1, 1)
             row_max(n, 1)
             row_max(n, 2)
-            if live(n + 1):
-                flip_x(n + 1)
             if live(n - 1):
                 e_mx[n - 1] = quantise(e_grouped[:], work, L, "e")
                 v_mx[n - 1] = quantise(v_grouped[:], work, H, "v")
@@ -429,9 +426,10 @@ def tile_relativeattentionhead_pa_kernel(tc, x, q, k, Wv, rel_emb, out):
             v_last = work.tile([P, H * PACK], BF16, name="v_grouped", align_bytes=64)
             nc.vector.tensor_copy(out=v_last[:].rearrange("p (h t) -> p h t", t=PACK), in_=v_ps[n][:].rearrange("p t h -> p h t"))
             weighted_sum(n - 1)
-            unload_e(n, (0,))
             unload_e(n, (1,))
             v_mx[n] = quantise(v_last[:], work, H, "v")
+            words = e_grouped[:].bitcast(F32).rearrange("p (k g i u) -> p k g i u", k=2, g=2, u=2)
+            nc.vector.tensor_copy(out=words[:, 0], in_=eT_banks[0][:].rearrange("p g u i -> p g i u"))
             invert_sums(n)
             finish_last()
 
@@ -445,11 +443,22 @@ def tile_relativeattentionhead_pa_kernel(tc, x, q, k, Wv, rel_emb, out):
         with tc.psum_pool(name="ps_head", bufs=8) as ps_head:
             keep_warm(ps_head.tile([P, BANK], F32, name="warm", tag="flip")[:], 5)
             unload_tokens(relT[:], flip_tokens(ps_head, rel_sb))
-            for first, stop in Q_LOADS:
-                for b in range(first, stop):
-                    unload_tokens(qT[b][:], flip_tokens(ps_head, q_sb[:, b * NBLK : (b + 1) * NBLK, :]))
-                for b in range(first, stop):
-                    make_rows(ps_head, b)
+            unload_tokens(qT[0][:], flip_tokens(ps_head, q_sb[:, 0 * NBLK : (0 + 1) * NBLK, :]))
+            unload_tokens(qT[1][:], flip_tokens(ps_head, q_sb[:, 1 * NBLK : (1 + 1) * NBLK, :]))
+            make_rows(ps_head, 0)
+            unload_tokens(qT[2][:], flip_tokens(ps_head, q_sb[:, 2 * NBLK : (2 + 1) * NBLK, :]))
+            make_rows(ps_head, 1)
+            unload_tokens(qT[3][:], flip_tokens(ps_head, q_sb[:, 3 * NBLK : (3 + 1) * NBLK, :]))
+            make_rows(ps_head, 2)
+            unload_tokens(qT[4][:], flip_tokens(ps_head, q_sb[:, 4 * NBLK : (4 + 1) * NBLK, :]))
+            make_rows(ps_head, 3)
+            unload_tokens(qT[5][:], flip_tokens(ps_head, q_sb[:, 5 * NBLK : (5 + 1) * NBLK, :]))
+            make_rows(ps_head, 4)
+            unload_tokens(qT[6][:], flip_tokens(ps_head, q_sb[:, 6 * NBLK : (6 + 1) * NBLK, :]))
+            make_rows(ps_head, 5)
+            unload_tokens(qT[7][:], flip_tokens(ps_head, q_sb[:, 7 * NBLK : (7 + 1) * NBLK, :]))
+            make_rows(ps_head, 6)
+            make_rows(ps_head, 7)
             for b in range(2):
                 nc.vector.tensor_copy(out=kT[b][:].rearrange("p (r g) -> p r g", g=NBLK), in_=flip_tokens(ps_head, k_sb[:, b * NBLK : (b + 1) * NBLK, :])[:].rearrange("p g r -> p r g"))
             wv_grouped = keep.tile([P, H * PACK], BF16, align_bytes=64)
@@ -462,11 +471,11 @@ def tile_relativeattentionhead_pa_kernel(tc, x, q, k, Wv, rel_emb, out):
         load_x(0)
         store_rows(0)
         store_rows(1)
-        load_rows(k_sb, k, 2, 3)
-        read_back(0)
         load_x(1)
+        read_back(0)
+        load_rows(k_sb, k, 2, 2 + 1)
         store_rows(2)
-        load_rows(k_sb, k, 3, 4)
+        load_rows(k_sb, k, 3, 3 + 1)
         read_back(1)
         for b in range(2, B):
             if live(b + 1):

@@ -392,7 +392,7 @@ def tile_relativeattentionhead_pa_kernel(tc, x, q, k, Wv, rel_emb, out):
             x_mx[n] = quantise(x_grouped[n][:], work, L, "x")
             exponentiate(n)
             if live(n + 2):
-                nc.scalar.copy(out=kT[n + 2][:].rearrange("p (r g) -> p r g", g=NBLK), in_=k_flipped[:].rearrange("p g r -> p r g"))
+                nc.scalar.copy(out=kT[n + 2][:], in_=k_flipped[:].rearrange("p g r -> p (g r)"))
             if live(n - 1):
                 invert_sums(n - 1)
 
@@ -436,31 +436,31 @@ def tile_relativeattentionhead_pa_kernel(tc, x, q, k, Wv, rel_emb, out):
 
         nc.sync.dma_start(out=rel_sb[:], in_=rel_emb.rearrange("(g p) h -> p g h", p=P))
         for first, stop in Q_LOADS:
-            load_tokens(q_sb, q, first, stop)
-        load_rows(k_sb, k, 0, 2)
+            load_rows(q_sb, q, first, stop)
+        load_tokens(k_sb, k, 0, 2)
         nc.sync.dma_start(out=wv_sb[:], in_=Wv)
 
         with tc.psum_pool(name="ps_head", bufs=8) as ps_head:
             keep_warm(ps_head.tile([P, BANK], F32, name="warm", tag="flip")[:], 5)
             unload_tokens(relT[:], flip_tokens(ps_head, rel_sb))
-            unload_tokens(qT[0][:], flip_tokens(ps_head, q_sb[:, 0 * NBLK : (0 + 1) * NBLK, :]))
-            unload_tokens(qT[1][:], flip_tokens(ps_head, q_sb[:, 1 * NBLK : (1 + 1) * NBLK, :]))
+            nc.vector.tensor_copy(out=qT[0][:].rearrange("p (r g) -> p r g", g=NBLK), in_=flip_tokens(ps_head, q_sb[:, 0 * NBLK : (0 + 1) * NBLK, :])[:].rearrange("p g r -> p r g"))
+            nc.vector.tensor_copy(out=qT[1][:].rearrange("p (r g) -> p r g", g=NBLK), in_=flip_tokens(ps_head, q_sb[:, 1 * NBLK : (1 + 1) * NBLK, :])[:].rearrange("p g r -> p r g"))
             make_rows(ps_head, 0)
-            unload_tokens(qT[2][:], flip_tokens(ps_head, q_sb[:, 2 * NBLK : (2 + 1) * NBLK, :]))
+            nc.vector.tensor_copy(out=qT[2][:].rearrange("p (r g) -> p r g", g=NBLK), in_=flip_tokens(ps_head, q_sb[:, 2 * NBLK : (2 + 1) * NBLK, :])[:].rearrange("p g r -> p r g"))
             make_rows(ps_head, 1)
-            unload_tokens(qT[3][:], flip_tokens(ps_head, q_sb[:, 3 * NBLK : (3 + 1) * NBLK, :]))
+            nc.vector.tensor_copy(out=qT[3][:].rearrange("p (r g) -> p r g", g=NBLK), in_=flip_tokens(ps_head, q_sb[:, 3 * NBLK : (3 + 1) * NBLK, :])[:].rearrange("p g r -> p r g"))
             make_rows(ps_head, 2)
-            unload_tokens(qT[4][:], flip_tokens(ps_head, q_sb[:, 4 * NBLK : (4 + 1) * NBLK, :]))
+            nc.vector.tensor_copy(out=qT[4][:].rearrange("p (r g) -> p r g", g=NBLK), in_=flip_tokens(ps_head, q_sb[:, 4 * NBLK : (4 + 1) * NBLK, :])[:].rearrange("p g r -> p r g"))
             make_rows(ps_head, 3)
-            unload_tokens(qT[5][:], flip_tokens(ps_head, q_sb[:, 5 * NBLK : (5 + 1) * NBLK, :]))
+            nc.vector.tensor_copy(out=qT[5][:].rearrange("p (r g) -> p r g", g=NBLK), in_=flip_tokens(ps_head, q_sb[:, 5 * NBLK : (5 + 1) * NBLK, :])[:].rearrange("p g r -> p r g"))
             make_rows(ps_head, 4)
-            unload_tokens(qT[6][:], flip_tokens(ps_head, q_sb[:, 6 * NBLK : (6 + 1) * NBLK, :]))
+            nc.vector.tensor_copy(out=qT[6][:].rearrange("p (r g) -> p r g", g=NBLK), in_=flip_tokens(ps_head, q_sb[:, 6 * NBLK : (6 + 1) * NBLK, :])[:].rearrange("p g r -> p r g"))
             make_rows(ps_head, 5)
-            unload_tokens(qT[7][:], flip_tokens(ps_head, q_sb[:, 7 * NBLK : (7 + 1) * NBLK, :]))
+            nc.vector.tensor_copy(out=qT[7][:].rearrange("p (r g) -> p r g", g=NBLK), in_=flip_tokens(ps_head, q_sb[:, 7 * NBLK : (7 + 1) * NBLK, :])[:].rearrange("p g r -> p r g"))
             make_rows(ps_head, 6)
             make_rows(ps_head, 7)
             for b in range(2):
-                nc.vector.tensor_copy(out=kT[b][:].rearrange("p (r g) -> p r g", g=NBLK), in_=flip_tokens(ps_head, k_sb[:, b * NBLK : (b + 1) * NBLK, :])[:].rearrange("p g r -> p r g"))
+                unload_tokens(kT[b][:], flip_tokens(ps_head, k_sb[:, b * NBLK : (b + 1) * NBLK, :]))
             wv_grouped = keep.tile([P, H * PACK], BF16, align_bytes=64)
             unload_features(
                 wv_grouped[:].bitcast(F32).rearrange("p (g r u) -> p g r u", g=1, u=2),
@@ -473,16 +473,16 @@ def tile_relativeattentionhead_pa_kernel(tc, x, q, k, Wv, rel_emb, out):
         store_rows(1)
         load_x(1)
         read_back(0)
-        load_rows(k_sb, k, 2, 2 + 1)
+        load_tokens(k_sb, k, 2, 2 + 1)
         store_rows(2)
-        load_rows(k_sb, k, 3, 3 + 1)
+        load_tokens(k_sb, k, 3, 3 + 1)
         read_back(1)
         for b in range(2, B):
             if live(b + 1):
                 store_rows(b + 1)
             load_x(b)
             if live(b + 2):
-                load_rows(k_sb, k, b + 2, b + 3)
+                load_tokens(k_sb, k, b + 2, b + 3)
             read_back(b)
 
         ps_flip = ctx.enter_context(tc.psum_pool(name="ps_flip", bufs=3, reuse_waits="tile"))

@@ -57,6 +57,7 @@ def tile_relativeattentionhead_pa_kernel(tc, x, q, k, Wv, rel_emb, out):
         ident_f32 = keep.tile([P, P], F32)
         mask_f32 = keep.tile([P, P], F32)
         mask_bf = keep.tile([P, P], BF16)
+        ident_scaled = keep.tile([P, P], F32)
         rel_sb = keep.tile([P, NBLK, H], BF16)
         wv_sb = keep.tile([P, E], BF16)
         q_sb = keep.tile([P, B * NBLK, H], BF16)
@@ -92,6 +93,7 @@ def tile_relativeattentionhead_pa_kernel(tc, x, q, k, Wv, rel_emb, out):
             for blk in (2, 0):
                 nc.vector.memset(es[:, E_COL0[blk] + WIDTH[blk] : E_COL0[blk] + WIDTH[blk] + P], 0.0)
         nc.vector.tensor_copy(out=mask_bf[:], in_=mask_f32[:])
+        nc.vector.tensor_scalar(out=ident_scaled[:], in0=ident_f32[:], scalar1=math.sqrt(H), scalar2=None, op0=ALU.mult)
 
         def load_rows(dst, src, first, stop):
             nc.sync.dma_start(
@@ -183,6 +185,8 @@ def tile_relativeattentionhead_pa_kernel(tc, x, q, k, Wv, rel_emb, out):
         e_mx = {}
         o_ps = {}
         neg_max = {}
+        neg_max1 = {}
+        bias1 = {}
         row_sum = {}
         inv_sum = {}
 
@@ -201,7 +205,7 @@ def tile_relativeattentionhead_pa_kernel(tc, x, q, k, Wv, rel_emb, out):
             if b < B - 1:
                 v_ps[b] = ps_mx.tile([P, NBLK, H], F32, name="v_ps", tag="mx")
             else:
-                v_ps[b] = ps_score.tile([P, NBLK, H], F32, name="v_ps", tag="score")
+                v_ps[b] = ps_score.tile([P, NBLK, H], F32, name="v_ps", tag="qk_ps0")
             x_words, x_scales = x_mx[b]
             for t in range(NBLK):
                 nc.tensor.matmul_mx(
@@ -225,13 +229,25 @@ def tile_relativeattentionhead_pa_kernel(tc, x, q, k, Wv, rel_emb, out):
         def scores(b, bank):
             blocks = BANKS[bank]
             first = COL0[blocks[0]]
-            qk_ps[b, bank] = ps_score.tile([P, BANK], F32, name="qk_ps", tag="score")
+            qk_ps[b, bank] = ps_score.tile([P, BANK], F32, name="qk_ps%d" % bank)
+            if bank == 2:
+                out = qk_ps[b, 2][:, 0 : 2 * P]
+                nc.tensor.matmul(out, lhsT=qT[b][:, P : 2 * P], rhs=kT[b][:, 0 : 2 * P], start=True, stop=False)
+                nc.tensor.matmul(out[:, P : 2 * P], lhsT=ident_bf[:], rhs=mask_bf[:], start=False, stop=False)
+                nc.tensor.matmul(out, lhsT=ident_scaled[:], rhs=s_sb[b][:, COL0[1] : COL0[1] + 2 * P], start=False, stop=True)
+                return
             for blk in blocks:
                 lo = COL0[blk] - first
                 queries = qT[b][:, blk * P : (blk + 1) * P]
                 out = qk_ps[b, bank][:, lo : lo + WIDTH[blk]]
                 nc.tensor.matmul(out, lhsT=queries, rhs=kT[b][:, 0 : WIDTH[blk]], start=True, stop=False)
                 nc.tensor.matmul(out[:, blk * P : WIDTH[blk]], lhsT=ident_bf[:], rhs=mask_bf[:], start=False, stop=True)
+
+        def flip_k(b):
+            planes = eT_banks[0][:].rearrange("p g u i -> p (g u i)").bitcast(BF16)[:, 0:L].rearrange("p (g r) -> p g r", g=NBLK)
+            for g in range(NBLK):
+                nc.tensor.transpose(planes[:, g, :], k_sb[:, b * NBLK + g, :], ident_bf[:])
+            nc.scalar.copy(out=kT[b][:], in_=planes.rearrange("p g r -> p (g r)"))
 
         def add_rel(b, bank):
             blocks = BANKS[bank]
@@ -249,6 +265,12 @@ def tile_relativeattentionhead_pa_kernel(tc, x, q, k, Wv, rel_emb, out):
             )
 
         def row_max(b, bank):
+            if bank == 2:
+                neg_max1[b] = small.tile([P, 1], F32, name="neg_max1")
+                bias1[b] = small.tile([P, 1], F32, name="bias1")
+                nc.vector.tensor_reduce(out=neg_max1[b][:], in_=qk_ps[b, 2][:, 0 : 2 * P], axis=AXIS.X, op=ALU.max, negate=True)
+                nc.gpsimd.tensor_scalar(out=bias1[b][:], in0=neg_max1[b][:], scalar1=SCALE, scalar2=0.0, op0=ALU.mult, op1=ALU.add)
+                return
             for blk in BANKS[bank]:
                 nc.vector.tensor_reduce(
                     out=neg_max[b][:, blk : blk + 1],
@@ -267,10 +289,10 @@ def tile_relativeattentionhead_pa_kernel(tc, x, q, k, Wv, rel_emb, out):
                     cols = slice(COL0[blk], COL0[blk] + WIDTH[blk])
                     nc.scalar.activation(
                         out=e_sb[b][:, E_COL0[blk] : E_COL0[blk] + WIDTH[blk]],
-                        in_=s_sb[b][:, cols],
+                        in_=qk_ps[b, 2][:, 0 : 2 * P] if blk == 1 else s_sb[b][:, cols],
                         func=ACT.Exp,
-                        bias=neg_max[b][:, blk : blk + 1],
-                        scale=1.0,
+                        bias=bias1[b][:] if blk == 1 else neg_max[b][:, blk : blk + 1],
+                        scale=SCALE if blk == 1 else 1.0,
                         accum_out=row_sum[b][:, blk : blk + 1],
                     )
                     for u in range(1 + blk // 2):
@@ -299,7 +321,7 @@ def tile_relativeattentionhead_pa_kernel(tc, x, q, k, Wv, rel_emb, out):
                 )
             store(b - 1, b)
             o_half = []
-            for bank, pool, tag in ((0, ps_score, "score"), (1, ps_flip, "flip")):
+            for bank, pool, tag in ((0, ps_score, "qk_ps1"), (1, ps_flip, "flip")):
                 e_words, e_scales = halves[bank]
                 o = pool.tile([P, 2, H], F32, name="o_half", tag=tag)
                 for i in range(2):
@@ -361,14 +383,10 @@ def tile_relativeattentionhead_pa_kernel(tc, x, q, k, Wv, rel_emb, out):
             return 0 <= b < B
 
         def step(n):
-            if live(n):
-                x_grouped[n] = unload_x(n)
+            x_grouped[n] = unload_x(n)
             if live(n - 1):
                 unload_e(n - 1)
-            if live(n + 2):
-                k_flipped = flip_tokens(ps_flip, k_sb[:, (n + 2) * NBLK : (n + 3) * NBLK, :])
             add_rel(n, 0)
-            scores(n, 2)
             if live(n - 2):
                 normalise(n - 2)
                 store_results(n - 2)
@@ -376,13 +394,12 @@ def tile_relativeattentionhead_pa_kernel(tc, x, q, k, Wv, rel_emb, out):
                 project(n - 1)
                 v_grouped = unload_v(n - 1)
             add_rel(n, 1)
-            if live(n + 1):
-                scores(n + 1, 0)
-                flip_x(n + 1)
+            scores(n + 1, 0)
+            if live(n + 2):
+                flip_k(n + 2)
+            flip_x(n + 1)
             row_max(n, 0)
-            add_rel(n, 2)
-            if live(n + 1):
-                scores(n + 1, 1)
+            scores(n + 1, 1)
             row_max(n, 1)
             row_max(n, 2)
             if live(n - 1):
@@ -391,8 +408,7 @@ def tile_relativeattentionhead_pa_kernel(tc, x, q, k, Wv, rel_emb, out):
                 weighted_sum(n - 1)
             x_mx[n] = quantise(x_grouped[n][:], work, L, "x")
             exponentiate(n)
-            if live(n + 2):
-                nc.scalar.copy(out=kT[n + 2][:], in_=k_flipped[:].rearrange("p g r -> p (g r)"))
+            scores(n + 1, 2)
             if live(n - 1):
                 invert_sums(n - 1)
 
@@ -407,7 +423,6 @@ def tile_relativeattentionhead_pa_kernel(tc, x, q, k, Wv, rel_emb, out):
             x_grouped[n] = unload_x(n)
             unload_e(n - 1)
             add_rel(n, 0)
-            scores(n, 2)
             normalise(n - 2)
             store_results(n - 2)
             project(n - 1)
@@ -415,7 +430,6 @@ def tile_relativeattentionhead_pa_kernel(tc, x, q, k, Wv, rel_emb, out):
             add_rel(n, 1)
             row_max(n, 0)
             x_mx[n] = quantise(x_grouped[n][:], work, L, "x")
-            add_rel(n, 2)
             row_max(n, 1)
             row_max(n, 2)
             project(n)
@@ -485,8 +499,8 @@ def tile_relativeattentionhead_pa_kernel(tc, x, q, k, Wv, rel_emb, out):
                 load_tokens(k_sb, k, b + 2, b + 3)
             read_back(b)
 
-        ps_flip = ctx.enter_context(tc.psum_pool(name="ps_flip", bufs=3, reuse_waits="tile"))
-        ps_score = ctx.enter_context(tc.psum_pool(name="ps_score", bufs=2, reuse_waits="tile"))
+        ps_flip = ctx.enter_context(tc.psum_pool(name="ps_flip", bufs=2, reuse_waits="tile"))
+        ps_score = ctx.enter_context(tc.psum_pool(name="ps_score", bufs=1, reuse_waits="tile"))
         ps_eT = ctx.enter_context(tc.psum_pool(name="ps_eT", bufs=1, reuse_waits="tile"))
         ps_mx = ctx.enter_context(tc.psum_pool(name="ps_mx", bufs=1, reuse_waits="tile"))
         eT_banks = [ps_eT.tile([P, 2, 2, P], F32, name="eT_bank%d" % i) for i in range(2)]
@@ -496,6 +510,7 @@ def tile_relativeattentionhead_pa_kernel(tc, x, q, k, Wv, rel_emb, out):
         scores(0, 0)
         scores(0, 1)
         flip_x(0)
+        scores(0, 2)
         for n in range(B - 1):
             step(n)
         last_step()

@@ -449,28 +449,31 @@ def tile_relativeattentionhead_pa_kernel(tc, x, q, k, Wv, rel_emb, out):
 
 
         nc.sync.dma_start(out=rel_sb[:], in_=rel_emb.rearrange("(g p) h -> p g h", p=P))
-        for first, stop in Q_LOADS:
-            load_rows(q_sb, q, first, stop)
+        load_rows(q_sb, q, 0, 1)
+        load_rows(q_sb, q, 1, 2)
+        load_rows(q_sb, q, 2, 3)
+        load_rows(q_sb, q, 3, 5)
+        load_rows(q_sb, q, 5, 8)
         load_tokens(k_sb, k, 0, 2)
         nc.sync.dma_start(out=wv_sb[:], in_=Wv)
 
         with tc.psum_pool(name="ps_head", bufs=8) as ps_head:
-            keep_warm(ps_head.tile([P, BANK], F32, name="warm", tag="flip")[:], 5)
+            keep_warm(ps_head.tile([P, BANK], F32, name="warm", tag="flip")[:], 3)
             unload_tokens(relT[:], flip_tokens(ps_head, rel_sb))
             nc.vector.tensor_copy(out=qT[0][:].rearrange("p (r g) -> p r g", g=NBLK), in_=flip_tokens(ps_head, q_sb[:, 0 * NBLK : (0 + 1) * NBLK, :])[:].rearrange("p g r -> p r g"))
             nc.vector.tensor_copy(out=qT[1][:].rearrange("p (r g) -> p r g", g=NBLK), in_=flip_tokens(ps_head, q_sb[:, 1 * NBLK : (1 + 1) * NBLK, :])[:].rearrange("p g r -> p r g"))
-            make_rows(ps_head, 0)
             nc.vector.tensor_copy(out=qT[2][:].rearrange("p (r g) -> p r g", g=NBLK), in_=flip_tokens(ps_head, q_sb[:, 2 * NBLK : (2 + 1) * NBLK, :])[:].rearrange("p g r -> p r g"))
-            make_rows(ps_head, 1)
+            make_rows(ps_head, 0)
             nc.vector.tensor_copy(out=qT[3][:].rearrange("p (r g) -> p r g", g=NBLK), in_=flip_tokens(ps_head, q_sb[:, 3 * NBLK : (3 + 1) * NBLK, :])[:].rearrange("p g r -> p r g"))
-            make_rows(ps_head, 2)
+            make_rows(ps_head, 1)
             nc.vector.tensor_copy(out=qT[4][:].rearrange("p (r g) -> p r g", g=NBLK), in_=flip_tokens(ps_head, q_sb[:, 4 * NBLK : (4 + 1) * NBLK, :])[:].rearrange("p g r -> p r g"))
-            make_rows(ps_head, 3)
+            make_rows(ps_head, 2)
             nc.vector.tensor_copy(out=qT[5][:].rearrange("p (r g) -> p r g", g=NBLK), in_=flip_tokens(ps_head, q_sb[:, 5 * NBLK : (5 + 1) * NBLK, :])[:].rearrange("p g r -> p r g"))
-            make_rows(ps_head, 4)
+            make_rows(ps_head, 3)
             nc.vector.tensor_copy(out=qT[6][:].rearrange("p (r g) -> p r g", g=NBLK), in_=flip_tokens(ps_head, q_sb[:, 6 * NBLK : (6 + 1) * NBLK, :])[:].rearrange("p g r -> p r g"))
-            make_rows(ps_head, 5)
+            make_rows(ps_head, 4)
             nc.vector.tensor_copy(out=qT[7][:].rearrange("p (r g) -> p r g", g=NBLK), in_=flip_tokens(ps_head, q_sb[:, 7 * NBLK : (7 + 1) * NBLK, :])[:].rearrange("p g r -> p r g"))
+            make_rows(ps_head, 5)
             make_rows(ps_head, 6)
             make_rows(ps_head, 7)
             for b in range(2):
@@ -483,11 +486,11 @@ def tile_relativeattentionhead_pa_kernel(tc, x, q, k, Wv, rel_emb, out):
             wv_words, wv_scales = quantise(wv_grouped[:], keep, H, "wv")
 
         load_x(0)
+        load_x(1)
         store_rows(0)
         store_rows(1)
-        load_x(1)
-        read_back(0)
         load_tokens(k_sb, k, 2, 2 + 1)
+        read_back(0)
         store_rows(2)
         load_tokens(k_sb, k, 3, 3 + 1)
         read_back(1)

@@ -52,7 +52,7 @@ def tile_relativeattentionhead_pa_kernel(tc, x, q, k, Wv, rel_emb, out):
         small = ctx.enter_context(tc.tile_pool(name="small", bufs=4))
         ctx.enter_context(tc.manual_schedule())
 
-        idle_bf = keep.tile([P, BANK], BF16)
+        idle_bf = keep.tile([P, P], BF16)
         ident_bf = keep.tile([P, P], BF16)
         ident_f32 = keep.tile([P, P], F32)
         mask_f32 = keep.tile([P, P], F32)
@@ -136,7 +136,7 @@ def tile_relativeattentionhead_pa_kernel(tc, x, q, k, Wv, rel_emb, out):
 
         def keep_warm(tile, times):
             for i in range(times):
-                nc.tensor.matmul(tile, lhsT=idle_bf[:, 0:P], rhs=idle_bf[:], start=True, stop=True)
+                nc.tensor.matmul(tile, lhsT=idle_bf[:], rhs=idle_bf[:, 0:1].to_broadcast([P, BANK]), start=True, stop=True)
 
         def flip_features(pool, src_words, n_groups, warm=0):
             flipped = pool.tile([P, n_groups, 2, P], F32, tag="flip")
@@ -407,6 +407,8 @@ def tile_relativeattentionhead_pa_kernel(tc, x, q, k, Wv, rel_emb, out):
                 v_mx[n - 1] = quantise(v_grouped[:], work, H, "v")
                 weighted_sum(n - 1)
             x_mx[n] = quantise(x_grouped[n][:], work, L, "x")
+            if n == 0:
+                keep_warm(ps_mx.tile([P, BANK], F32, name="warm", tag="mx")[:], 1)
             exponentiate(n)
             scores(n + 1, 2)
             if live(n - 1):
@@ -433,6 +435,7 @@ def tile_relativeattentionhead_pa_kernel(tc, x, q, k, Wv, rel_emb, out):
             row_max(n, 1)
             row_max(n, 2)
             project(n)
+            keep_warm(ps_flip.tile([P, BANK], F32, name="warm", tag="flip")[:], 2)
             e_mx[n - 1] = quantise(e_grouped[:], work, L, "e")
             v_mx[n - 1] = quantise(v_grouped[:], work, H, "v")
             exponentiate(n)
@@ -440,6 +443,7 @@ def tile_relativeattentionhead_pa_kernel(tc, x, q, k, Wv, rel_emb, out):
             v_last = work.tile([P, H * PACK], BF16, name="v_grouped", align_bytes=64)
             nc.vector.tensor_copy(out=v_last[:].rearrange("p (h t) -> p h t", t=PACK), in_=v_ps[n][:].rearrange("p t h -> p h t"))
             weighted_sum(n - 1)
+            keep_warm(ps_flip.tile([P, BANK], F32, name="warm", tag="flip")[:], 1)
             unload_e(n, (1,))
             v_mx[n] = quantise(v_last[:], work, H, "v")
             words = e_grouped[:].bitcast(F32).rearrange("p (k g i u) -> p k g i u", k=2, g=2, u=2)
@@ -458,9 +462,10 @@ def tile_relativeattentionhead_pa_kernel(tc, x, q, k, Wv, rel_emb, out):
         nc.sync.dma_start(out=wv_sb[:], in_=Wv)
 
         with tc.psum_pool(name="ps_head", bufs=8) as ps_head:
-            keep_warm(ps_head.tile([P, BANK], F32, name="warm", tag="flip")[:], 3)
+            keep_warm(ps_head.tile([P, BANK], F32, name="warm", tag="flip")[:], 4)
             unload_tokens(relT[:], flip_tokens(ps_head, rel_sb))
             nc.vector.tensor_copy(out=qT[0][:].rearrange("p (r g) -> p r g", g=NBLK), in_=flip_tokens(ps_head, q_sb[:, 0 * NBLK : (0 + 1) * NBLK, :])[:].rearrange("p g r -> p r g"))
+            keep_warm(ps_head.tile([P, BANK], F32, name="warm", tag="flip")[:], 1)
             nc.vector.tensor_copy(out=qT[1][:].rearrange("p (r g) -> p r g", g=NBLK), in_=flip_tokens(ps_head, q_sb[:, 1 * NBLK : (1 + 1) * NBLK, :])[:].rearrange("p g r -> p r g"))
             nc.vector.tensor_copy(out=qT[2][:].rearrange("p (r g) -> p r g", g=NBLK), in_=flip_tokens(ps_head, q_sb[:, 2 * NBLK : (2 + 1) * NBLK, :])[:].rearrange("p g r -> p r g"))
             make_rows(ps_head, 0)

import math
from contextlib import ExitStack

import concourse.mybir as mybir
from concourse.masks import make_identity

F32 = mybir.dt.float32
BF16 = mybir.dt.bfloat16
U32 = mybir.dt.uint32
U8 = mybir.dt.uint8
FP8X4 = mybir.dt.float8_e4m3fn_x4
ALU = mybir.AluOpType
ACT = mybir.ActivationFunctionType
AXIS = mybir.AxisListType

B, L, E, H = 8, 512, 512, 128
P = 128
PACK = 4
NBLK = L // P
BANK = 512

FLOPS = 4 * 2 * B * L * L * H

WIDTH = {0: 128, 1: 256, 2: 384, 3: 512}
BANKS = ((3,), (2, 0), (1,))
COL0 = {3: 0, 2: 512, 0: 896, 1: 1024}
ROW = 1280
E_COL0 = {3: 0, 2: 512, 1: 1024, 0: 1280}
E_ROW = 1536
E_BANKS = ((3, 2), (1, 0))
PAD = 8
PITCH = ROW + PAD
SLOT = P * PITCH
N_SLOTS = 3
assert N_SLOTS * SLOT <= B * L * H

Q_LOADS = ((0, 1), (1, 3), (3, 5), (5, B))

MASKED = -1.0e30
SCALE = 1.0 / math.sqrt(H)

FIRST_STORE = 4


def tile_relativeattentionhead_pa_kernel(tc, x, q, k, Wv, rel_emb, out):
    nc = tc.nc
    out_flat = out.rearrange("b l h -> (b l h)")

    with ExitStack() as ctx:
        keep = ctx.enter_context(tc.tile_pool(name="keep", bufs=1))
        work = ctx.enter_context(tc.tile_pool(name="work", bufs=2))
        small = ctx.enter_context(tc.tile_pool(name="small", bufs=4))
        ctx.enter_context(tc.manual_schedule())

        idle_bf = keep.tile([P, P], BF16)
        ident_bf = keep.tile([P, P], BF16)
        ident_f32 = keep.tile([P, P], F32)
        mask_f32 = keep.tile([P, P], F32)
        mask_bf = keep.tile([P, P], BF16)
        ident_scaled = keep.tile([P, P], F32)
        rel_sb = keep.tile([P, NBLK, H], BF16)
        wv_sb = keep.tile([P, E], BF16)
        q_sb = keep.tile([P, B * NBLK, H], BF16)
        k_sb = keep.tile([P, B * NBLK, H], BF16)
        x_sb = keep.tile([P, B * NBLK, E], BF16)
        relT = keep.tile([P, L], BF16)
        qT = [keep.tile([P, L], BF16, name="qT%d" % b) for b in range(B)]
        kT = [keep.tile([P, L], BF16, name="kT%d" % b) for b in range(B)]
        m_rows = [keep.tile([P, PITCH], F32, name="m_rows%d" % b) for b in range(B)]
        s_sb = [keep.tile([P, ROW], F32, name="s_sb%d" % b) for b in range(B)]
        e_grouped = keep.tile([P, NBLK * P * PACK], BF16, align_bytes=64)
        e_sbs = [keep.tile([P, E_ROW], BF16, name="e_sb%d" % i) for i in range(2)]
        zero_f32 = keep.tile([P, P], F32)
        out_sb = keep.tile([P, B * NBLK, H], F32)

        nc.vector.memset(idle_bf[:], 0.0)
        make_identity(nc, ident_bf[:])
        nc.gpsimd.memset(mask_f32[:], 0.0)
        nc.gpsimd.affine_select(
            out=mask_f32[:],
            in_=mask_f32[:],
            compare_op=ALU.is_ge,
            fill=MASKED,
            base=0,
            pattern=[[-1, P]],
            channel_multiplier=1,
        )
        make_identity(nc, ident_f32[:])
        for rows in m_rows:
            nc.vector.memset(rows[:, ROW:PITCH], 0.0)
        nc.vector.memset(zero_f32[:], 0.0)
        for es in e_sbs:
            for blk in (2, 0):
                nc.vector.memset(es[:, E_COL0[blk] + WIDTH[blk] : E_COL0[blk] + WIDTH[blk] + P], 0.0)
        nc.vector.tensor_copy(out=mask_bf[:], in_=mask_f32[:])
        nc.vector.tensor_scalar(out=ident_scaled[:], in0=ident_f32[:], scalar1=math.sqrt(H), scalar2=None, op0=ALU.mult)

        def load_rows(dst, src, first, stop):
            nc.sync.dma_start(
                out=dst[:, first * NBLK : stop * NBLK, :].rearrange("p (b g) f -> p b (g f)", g=NBLK),
                in_=src[first:stop].rearrange("b (p g) f -> p b (g f)", p=P),
            )

        def load_tokens(dst, src, first, stop):
            nc.sync.dma_start(
                out=dst[:, first * NBLK : stop * NBLK, :],
                in_=src[first:stop].rearrange("b (g p) f -> p (b g) f", p=P),
            )

        def copy_out(piece, dst, src):
            if piece % 2 == 0:
                nc.scalar.copy(out=dst, in_=src)
            else:
                nc.vector.tensor_copy(out=dst, in_=src)

        def quantise(bf16_tile, pool, width, name):
            words = pool.tile([P, width], U32, name=name + "_words", align_bytes=64)
            scales = pool.tile([P, width], U8, name=name + "_scales", align_bytes=64)
            nc.vector.quantize_mx(out=words[:].bitcast(FP8X4), scales=scales[:], in_=bf16_tile)
            return words, scales

        def flip_tokens(pool, src):
            flipped = pool.tile([P, NBLK, P], BF16, tag="flip")
            for g in range(NBLK):
                nc.tensor.transpose(flipped[:, g, :], src[:, g, :], ident_bf[:])
            return flipped

        def load_x(b):
            nc.sync.dma_start(
                out=x_sb[:, b * NBLK : (b + 1) * NBLK, :].rearrange("p (u e) f -> p u (e f)", u=2),
                in_=x[b].rearrange("(u p e) f -> p u (e f)", u=2, e=2),
            )

        def unload_tokens(dst, flipped):
            nc.vector.tensor_copy(out=dst, in_=flipped[:].rearrange("p g r -> p (g r)"))

        def keep_warm(tile, times):
            for i in range(times):
                nc.tensor.matmul(tile, lhsT=idle_bf[:], rhs=idle_bf[:, 0:1].to_broadcast([P, BANK]), start=True, stop=True)

        def flip_features(pool, src_words, n_groups, warm=0):
            flipped = pool.tile([P, n_groups, 2, P], F32, tag="flip")
            if warm:
                keep_warm(flipped[:].rearrange("p g u r -> p (g u r)"), warm)
            for g in range(n_groups):
                for u in range(2):
                    nc.tensor.transpose(flipped[:, g, u, :], src_words[:, g, u * P : (u + 1) * P], ident_f32[:])
            return flipped

        def unload_features(dst_words, flipped):
            nc.scalar.copy(out=dst_words, in_=flipped[:].rearrange("p g u r -> p g r u"))

        def make_rows(pool, b):
            for bank, blocks in enumerate(BANKS):
                first = COL0[blocks[0]]
                m_ps = pool.tile([P, BANK], F32, tag="flip")
                for blk in blocks:
                    lo = COL0[blk] - first
                    nc.tensor.matmul(
                        m_ps[:, lo : lo + WIDTH[blk]],
                        lhsT=qT[b][:, blk * P : (blk + 1) * P],
                        rhs=relT[:, L - WIDTH[blk] : L],
                        start=True,
                        stop=True,
                    )
                width = sum(WIDTH[blk] for blk in blocks)
                copy_out(bank, m_rows[b][:, first : first + width], m_ps[:, 0:width])

        def store_rows(b):
            base = (b % N_SLOTS) * SLOT
            nc.sync.dma_start(out=out_flat[base : base + SLOT].rearrange("(p c) -> p c", c=PITCH), in_=m_rows[b][:])

        def read_back(b):
            base = (b % N_SLOTS) * SLOT + P - 1
            shifted = out_flat[base : base + P * (PITCH - 1)].rearrange("(p c) -> p c", c=PITCH - 1)
            nc.sync.dma_start(out=s_sb[b][:], in_=shifted[:, 0:ROW])

        x_flipped = {}
        x_mx = {}
        v_ps = {}
        v_mx = {}
        x_grouped = {}
        qk_ps = {}
        e_sb = {}
        e_mx = {}
        o_ps = {}
        neg_max = {}
        neg_max1 = {}
        bias1 = {}
        row_sum = {}
        inv_sum = {}

        def flip_x(b):
            src = x_sb[:].bitcast(F32)[:, b * NBLK : (b + 1) * NBLK, :]
            x_flipped[b] = [flip_features(ps_flip, src[:, 2 * half : 2 * half + 2, :], 2, 0) for half in range(2)]

        def unload_x(b):
            grouped = work.tile([P, L * PACK], BF16, name="x_grouped", align_bytes=64)
            dst = grouped[:].bitcast(F32).rearrange("p (g r u) -> p g r u", g=NBLK, u=2)
            for half in range(2):
                unload_features(dst[:, 2 * half : 2 * half + 2], x_flipped[b][half])
            return grouped

        def project(b):
            if b < B - 1:
                v_ps[b] = ps_mx.tile([P, NBLK, H], F32, name="v_ps", tag="mx")
            else:
                v_ps[b] = ps_score.tile([P, NBLK, H], F32, name="v_ps", tag="qk_ps0")
            x_words, x_scales = x_mx[b]
            for t in range(NBLK):
                nc.tensor.matmul_mx(
                    out=v_ps[b][:, t, :],
                    lhsT=x_words[:, t * P : (t + 1) * P].bitcast(FP8X4),
                    lhsT_scale=x_scales[:, t * P : (t + 1) * P],
                    rhs=wv_words[:].bitcast(FP8X4),
                    rhs_scale=wv_scales[:],
                    start=True,
                    stop=True,
                )

        def unload_v(b):
            v_grouped = work.tile([P, H * PACK], BF16, name="v_grouped", align_bytes=64)
            nc.scalar.copy(
                out=v_grouped[:].rearrange("p (h t) -> p h t", t=PACK),
                in_=v_ps[b][:].rearrange("p t h -> p h t"),
            )
            return v_grouped

        def scores(b, bank):
            blocks = BANKS[bank]
            first = COL0[blocks[0]]
            qk_ps[b, bank] = ps_score.tile([P, BANK], F32, name="qk_ps%d" % bank)
            if bank == 2:
                out = qk_ps[b, 2][:, 0 : 2 * P]
                nc.tensor.matmul(out, lhsT=qT[b][:, P : 2 * P], rhs=kT[b][:, 0 : 2 * P], start=True, stop=False)
                nc.tensor.matmul(out[:, P : 2 * P], lhsT=ident_bf[:], rhs=mask_bf[:], start=False, stop=False)
                nc.tensor.matmul(out, lhsT=ident_scaled[:], rhs=s_sb[b][:, COL0[1] : COL0[1] + 2 * P], start=False, stop=True)
                return
            for blk in blocks:
                lo = COL0[blk] - first
                queries = qT[b][:, blk * P : (blk + 1) * P]
                out = qk_ps[b, bank][:, lo : lo + WIDTH[blk]]
                nc.tensor.matmul(out, lhsT=queries, rhs=kT[b][:, 0 : WIDTH[blk]], start=True, stop=False)
                nc.tensor.matmul(out[:, blk * P : WIDTH[blk]], lhsT=ident_bf[:], rhs=mask_bf[:], start=False, stop=True)

        def flip_k(b):
            planes = eT_banks[0][:].rearrange("p g u i -> p (g u i)").bitcast(BF16)[:, 0:L].rearrange("p (g r) -> p g r", g=NBLK)
            for g in range(NBLK):
                nc.tensor.transpose(planes[:, g, :], k_sb[:, b * NBLK + g, :], ident_bf[:])
            nc.scalar.copy(out=kT[b][:], in_=planes.rearrange("p g r -> p (g r)"))

        def add_rel(b, bank):
            blocks = BANKS[bank]
            first = COL0[blocks[0]]
            width = sum(WIDTH[blk] for blk in blocks)
            if bank == 0:
                neg_max[b] = small.tile([P, NBLK], F32, name="neg_max")
            nc.vector.scalar_tensor_tensor(
                out=s_sb[b][:, first : first + width],
                in0=qk_ps[b, bank][:, 0:width],
                scalar=SCALE,
                in1=s_sb[b][:, first : first + width],
                op0=ALU.mult,
                op1=ALU.add,
            )

        def row_max(b, bank):
            if bank == 2:
                neg_max1[b] = small.tile([P, 1], F32, name="neg_max1")
                bias1[b] = small.tile([P, 1], F32, name="bias1")
                nc.vector.tensor_reduce(out=neg_max1[b][:], in_=qk_ps[b, 2][:, 0 : 2 * P], axis=AXIS.X, op=ALU.max, negate=True)
                nc.gpsimd.tensor_scalar(out=bias1[b][:], in0=neg_max1[b][:], scalar1=SCALE, scalar2=0.0, op0=ALU.mult, op1=ALU.add)
                return
            for blk in BANKS[bank]:
                nc.vector.tensor_reduce(
                    out=neg_max[b][:, blk : blk + 1],
                    in_=s_sb[b][:, COL0[blk] : COL0[blk] + WIDTH[blk]],
                    axis=AXIS.X,
                    op=ALU.max,
                    negate=True,
                )

        def exponentiate(b):
            e_sb[b] = e_sbs[b % 2]
            e_words = e_sb[b][:].bitcast(F32)
            row_sum[b] = small.tile([P, NBLK], F32, name="row_sum")
            for blocks in BANKS:
                for blk in blocks:
                    cols = slice(COL0[blk], COL0[blk] + WIDTH[blk])
                    nc.scalar.activation(
                        out=e_sb[b][:, E_COL0[blk] : E_COL0[blk] + WIDTH[blk]],
                        in_=qk_ps[b, 2][:, 0 : 2 * P] if blk == 1 else s_sb[b][:, cols],
                        func=ACT.Exp,
                        bias=bias1[b][:] if blk == 1 else neg_max[b][:, blk : blk + 1],
                        scale=SCALE if blk == 1 else 1.0,
                        accum_out=row_sum[b][:, blk : blk + 1],
                    )
                    for u in range(1 + blk // 2):
                        first = E_COL0[blk] // 2 + u * P
                        nc.tensor.transpose(eT_plane(blk, u), e_words[:, first : first + P], ident_f32[:])

        def eT_plane(blk, u):
            bank = 0 if blk in E_BANKS[0] else 1
            return eT_banks[bank][:, E_BANKS[bank].index(blk), u, :]

        def unload_e(b, banks=(0, 1)):
            words = e_grouped[:].bitcast(F32).rearrange("p (k g i u) -> p k g i u", k=2, g=2, u=2)
            for bank in banks:
                nc.scalar.copy(out=words[:, bank], in_=eT_banks[bank][:].rearrange("p g u i -> p g i u"))

        def finish_last():
            b = B - 1
            v_words, v_scales = v_mx[b]
            halves = [quantise(e_grouped[:, i * 2 * P * PACK : (i + 1) * 2 * P * PACK], work, 2 * P, "e_half") for i in range(2)]
            for blk in range(NBLK):
                nc.scalar.activation(
                    out=out_sb[:, (b - 1) * NBLK + blk, :],
                    in_=o_ps[b - 1][:, blk, :],
                    func=ACT.Copy,
                    scale=inv_sum[b - 1][:, blk : blk + 1],
                )
            store(b - 1, b)
            o_half = []
            for bank, pool, tag in ((0, ps_score, "qk_ps1"), (1, ps_flip, "flip")):
                e_words, e_scales = halves[bank]
                o = pool.tile([P, 2, H], F32, name="o_half", tag=tag)
                for i in range(2):
                    nc.tensor.matmul_mx(
                        out=o[:, 1 - i, :],
                        lhsT=e_words[:, i * P : (i + 1) * P].bitcast(FP8X4),
                        lhsT_scale=e_scales[:, i * P : (i + 1) * P],
                        rhs=v_words[:].bitcast(FP8X4),
                        rhs_scale=v_scales[:],
                        start=True,
                        stop=True,
                    )
                first = 2 * (1 - bank)
                nc.vector.tensor_tensor(
                    out=out_sb[:, b * NBLK + first : b * NBLK + first + 2, :],
                    in0=o[:],
                    in1=inv_sum[b][:, first : first + 2].unsqueeze(2).to_broadcast([P, 2, H]),
                    op=ALU.mult,
                )
                nc.sync.dma_start(
                    out=out[b, first * P : (first + 2) * P].rearrange("(g p) h -> p g h", p=P),
                    in_=out_sb[:, b * NBLK + first : b * NBLK + first + 2, :],
                )

        def weighted_sum(b):
            o_ps[b] = ps_mx.tile([P, NBLK, H], F32, name="o_ps", tag="mx")
            e_words, e_scales = e_mx[b]
            v_words, v_scales = v_mx[b]
            for blk in range(NBLK):
                nc.tensor.matmul_mx(
                    out=o_ps[b][:, blk, :],
                    lhsT=e_words[:, (3 - blk) * P : (4 - blk) * P].bitcast(FP8X4),
                    lhsT_scale=e_scales[:, (3 - blk) * P : (4 - blk) * P],
                    rhs=v_words[:].bitcast(FP8X4),
                    rhs_scale=v_scales[:],
                    start=True,
                    stop=True,
                )

        def invert_sums(b):
            inv_sum[b] = small.tile([P, NBLK], F32, name="inv_sum")
            nc.vector.reciprocal(out=inv_sum[b][:], in_=row_sum[b][:])

        def normalise(b):
            nc.vector.tensor_tensor(
                out=out_sb[:, b * NBLK : (b + 1) * NBLK, :],
                in0=o_ps[b][:],
                in1=inv_sum[b][:].unsqueeze(2).to_broadcast([P, NBLK, H]),
                op=ALU.mult,
            )

        def store(first, stop):
            nc.sync.dma_start(
                out=out[first:stop].rearrange("b (g p) h -> p (b g) h", p=P),
                in_=out_sb[:, first * NBLK : stop * NBLK, :],
            )

        def live(b):
            return 0 <= b < B

        def step(n):
            x_grouped[n] = unload_x(n)
            if live(n - 1):
                unload_e(n - 1)
            add_rel(n, 0)
            if live(n - 2):
                normalise(n - 2)
                store_results(n - 2)
            if live(n - 1):
                project(n - 1)
                v_grouped = unload_v(n - 1)
            add_rel(n, 1)
            scores(n + 1, 0)
            if live(n + 2):
                flip_k(n + 2)
            flip_x(n + 1)
            row_max(n, 0)
            scores(n + 1, 1)
            row_max(n, 1)
            row_max(n, 2)
            if live(n - 1):
                e_mx[n - 1] = quantise(e_grouped[:], work, L, "e")
                v_mx[n - 1] = quantise(v_grouped[:], work, H, "v")
                weighted_sum(n - 1)
            x_mx[n] = quantise(x_grouped[n][:], work, L, "x")
            if n == 0:
                keep_warm(ps_mx.tile([P, BANK], F32, name="warm", tag="mx")[:], 1)
            exponentiate(n)
            scores(n + 1, 2)
            if live(n - 1):
                invert_sums(n - 1)

        def store_results(b):
            if b == FIRST_STORE:
                store(0, b + 1)
            elif b > FIRST_STORE:
                store(b, b + 1)

        def last_step():
            n = B - 1
            x_grouped[n] = unload_x(n)
            unload_e(n - 1)
            add_rel(n, 0)
            normalise(n - 2)
            store_results(n - 2)
            project(n - 1)
            v_grouped = unload_v(n - 1)
            add_rel(n, 1)
            row_max(n, 0)
            x_mx[n] = quantise(x_grouped[n][:], work, L, "x")
            row_max(n, 1)
            row_max(n, 2)
            project(n)
            keep_warm(ps_flip.tile([P, BANK], F32, name="warm", tag="flip")[:], 2)
            e_mx[n - 1] = quantise(e_grouped[:], work, L, "e")
            v_mx[n - 1] = quantise(v_grouped[:], work, H, "v")
            exponentiate(n)
            invert_sums(n - 1)
            v_last = work.tile([P, H * PACK], BF16, name="v_grouped", align_bytes=64)
            nc.vector.tensor_copy(out=v_last[:].rearrange("p (h t) -> p h t", t=PACK), in_=v_ps[n][:].rearrange("p t h -> p h t"))
            weighted_sum(n - 1)
            keep_warm(ps_flip.tile([P, BANK], F32, name="warm", tag="flip")[:], 1)
            unload_e(n, (1,))
            v_mx[n] = quantise(v_last[:], work, H, "v")
            words = e_grouped[:].bitcast(F32).rearrange("p (k g i u) -> p k g i u", k=2, g=2, u=2)
            nc.vector.tensor_copy(out=words[:, 0], in_=eT_banks[0][:].rearrange("p g u i -> p g i u"))
            invert_sums(n)
            finish_last()


        nc.sync.dma_start(out=rel_sb[:], in_=rel_emb.rearrange("(g p) h -> p g h", p=P))
        load_rows(q_sb, q, 0, 1)
        load_rows(q_sb, q, 1, 2)
        load_rows(q_sb, q, 2, 3)
        load_rows(q_sb, q, 3, 5)
        load_rows(q_sb, q, 5, 8)
        load_tokens(k_sb, k, 0, 2)
        nc.sync.dma_start(out=wv_sb[:], in_=Wv)

        with tc.psum_pool(name="ps_head", bufs=8) as ps_head:
            keep_warm(ps_head.tile([P, BANK], F32, name="warm", tag="flip")[:], 4)
            unload_tokens(relT[:], flip_tokens(ps_head, rel_sb))
            nc.vector.tensor_copy(out=qT[0][:].rearrange("p (r g) -> p r g", g=NBLK), in_=flip_tokens(ps_head, q_sb[:, 0 * NBLK : (0 + 1) * NBLK, :])[:].rearrange("p g r -> p r g"))
            keep_warm(ps_head.tile([P, BANK], F32, name="warm", tag="flip")[:], 1)
            nc.vector.tensor_copy(out=qT[1][:].rearrange("p (r g) -> p r g", g=NBLK), in_=flip_tokens(ps_head, q_sb[:, 1 * NBLK : (1 + 1) * NBLK, :])[:].rearrange("p g r -> p r g"))
            nc.vector.tensor_copy(out=qT[2][:].rearrange("p (r g) -> p r g", g=NBLK), in_=flip_tokens(ps_head, q_sb[:, 2 * NBLK : (2 + 1) * NBLK, :])[:].rearrange("p g r -> p r g"))
            make_rows(ps_head, 0)
            nc.vector.tensor_copy(out=qT[3][:].rearrange("p (r g) -> p r g", g=NBLK), in_=flip_tokens(ps_head, q_sb[:, 3 * NBLK : (3 + 1) * NBLK, :])[:].rearrange("p g r -> p r g"))
            make_rows(ps_head, 1)
            nc.vector.tensor_copy(out=qT[4][:].rearrange("p (r g) -> p r g", g=NBLK), in_=flip_tokens(ps_head, q_sb[:, 4 * NBLK : (4 + 1) * NBLK, :])[:].rearrange("p g r -> p r g"))
            make_rows(ps_head, 2)
            nc.vector.tensor_copy(out=qT[5][:].rearrange("p (r g) -> p r g", g=NBLK), in_=flip_tokens(ps_head, q_sb[:, 5 * NBLK : (5 + 1) * NBLK, :])[:].rearrange("p g r -> p r g"))
            make_rows(ps_head, 3)
            nc.vector.tensor_copy(out=qT[6][:].rearrange("p (r g) -> p r g", g=NBLK), in_=flip_tokens(ps_head, q_sb[:, 6 * NBLK : (6 + 1) * NBLK, :])[:].rearrange("p g r -> p r g"))
            make_rows(ps_head, 4)
            nc.vector.tensor_copy(out=qT[7][:].rearrange("p (r g) -> p r g", g=NBLK), in_=flip_tokens(ps_head, q_sb[:, 7 * NBLK : (7 + 1) * NBLK, :])[:].rearrange("p g r -> p r g"))
            make_rows(ps_head, 5)
            make_rows(ps_head, 6)
            make_rows(ps_head, 7)
            for b in range(2):
                unload_tokens(kT[b][:], flip_tokens(ps_head, k_sb[:, b * NBLK : (b + 1) * NBLK, :]))
            wv_grouped = keep.tile([P, H * PACK], BF16, align_bytes=64)
            unload_features(
                wv_grouped[:].bitcast(F32).rearrange("p (g r u) -> p g r u", g=1, u=2),
                flip_features(ps_head, wv_sb[:].bitcast(F32).rearrange("p (g w) -> p g w", g=1), 1),
            )
            wv_words, wv_scales = quantise(wv_grouped[:], keep, H, "wv")

        load_x(0)
        load_x(1)
        store_rows(0)
        store_rows(1)
        load_tokens(k_sb, k, 2, 2 + 1)
        read_back(0)
        store_rows(2)
        load_tokens(k_sb, k, 3, 3 + 1)
        read_back(1)
        for b in range(2, B):
            if live(b + 1):
                store_rows(b + 1)
            load_x(b)
            if live(b + 2):
                load_tokens(k_sb, k, b + 2, b + 3)
            read_back(b)

        ps_flip = ctx.enter_context(tc.psum_pool(name="ps_flip", bufs=2, reuse_waits="tile"))
        ps_score = ctx.enter_context(tc.psum_pool(name="ps_score", bufs=1, reuse_waits="tile"))
        ps_eT = ctx.enter_context(tc.psum_pool(name="ps_eT", bufs=1, reuse_waits="tile"))
        ps_mx = ctx.enter_context(tc.psum_pool(name="ps_mx", bufs=1, reuse_waits="tile"))
        eT_banks = [ps_eT.tile([P, 2, 2, P], F32, name="eT_bank%d" % i) for i in range(2)]
        for g in range(2):
            nc.tensor.transpose(eT_banks[1][:, g, 1, :], zero_f32[:], ident_f32[:])

        scores(0, 0)
        scores(0, 1)
        flip_x(0)
        scores(0, 2)
        for n in range(B - 1):
            step(n)
        last_step()
